import numpy as np
import ml_dtypes


def mxq(x, axis, fmt="e4m3"):
    dtype, down = {"e4m3": (ml_dtypes.float8_e4m3fn, 7), "e5m2": (ml_dtypes.float8_e5m2, 14)}[fmt]
    v = np.moveaxis(np.asarray(x, np.float32).astype(ml_dtypes.bfloat16).astype(np.float64), axis, -1)
    blocks = v.reshape(v.shape[:-1] + (-1, 32))
    amax = np.abs(blocks).max(-1, keepdims=True)
    byte = np.maximum(np.where(amax > 0, np.frexp(amax)[1] - 1 + 127, 0) - down, 1)
    scale = np.exp2(byte - 127.0)
    codes = (blocks / scale).astype(np.float32).astype(dtype).astype(np.float64)
    return np.moveaxis((codes * scale).reshape(v.shape), -1, axis)


WIDE = False


def mx_kscale(k):
    if not WIDE:
        return np.ones(k)
    levels = np.array([10, -10, 5, -5, 0])
    a = np.random.permutation(np.resize(levels, k // 512 * 4)).reshape(k // 512, 4)
    idx = np.arange(k)
    return np.exp2(a[idx // 512, idx % 128 // 32])


BF16 = ml_dtypes.bfloat16


def bf(x):
    return np.asarray(x, np.float32).astype(BF16)


def f64(x):
    return np.asarray(x).astype(np.float64)


B, S, E, H, G, P, K3, K5, K7 = 2, 2048, 512, 8, 4, 3, 3, 5, 7
D = E // H
HK = H // G


def dwconv_causal(x, w, b):
    k = w.shape[1]
    xp = np.pad(x, ((0, 0), (0, 0), (k - 1, 0), (0, 0)))
    y = b
    for i in range(k):
        y = y + xp[:, :, i:i + S, :] * w[:, i]
    return y


def split_heads(t):
    return t.reshape(B, S, H, D).swapaxes(1, 2)


def tranception_mix(t, ws_bs):
    parts = [t[:, :HK]]
    for g, (w, b) in enumerate(ws_bs):
        parts.append(dwconv_causal(t[:, (g + 1) * HK:(g + 2) * HK], w, b))
    return np.concatenate(parts, axis=1)


def setup_inputs():
    s = mx_kscale(E)
    inp = {'hidden_states': bf(np.random.standard_normal((B, S, E)) * s),
           'c_attn_w': bf(np.random.standard_normal((E, P * E)) / np.sqrt(E) / s[:, None]),
           'c_attn_b': bf(np.random.standard_normal(P * E) * 0.3)}
    for pre in ('q', 'k', 'v'):
        for kern in (K3, K5, K7):
            inp[pre + 'w' + str(kern)] = bf(np.random.standard_normal((D, kern)) / kern)
            inp[pre + 'b' + str(kern)] = bf(np.random.standard_normal(D) * 0.2)
    return inp


def reference(hidden_states, c_attn_w, c_attn_b,
              qw3, qb3, qw5, qb5, qw7, qb7,
              kw3, kb3, kw5, kb5, kw7, kb7,
              vw3, vb3, vw5, vb5, vw7, vb7):
    qkv = (mxq(f64(hidden_states), 2, 'e4m3') @ mxq(f64(c_attn_w), 0, 'e4m3')) + f64(c_attn_b)
    q, k, v = np.split(qkv, P, axis=-1)
    q, k, v = split_heads(q), split_heads(k), split_heads(v)
    q = tranception_mix(q, [(f64(qw3), f64(qb3)), (f64(qw5), f64(qb5)), (f64(qw7), f64(qb7))])
    k = tranception_mix(k, [(f64(kw3), f64(kb3)), (f64(kw5), f64(kb5)), (f64(kw7), f64(kb7))])
    v = tranception_mix(v, [(f64(vw3), f64(vb3)), (f64(vw5), f64(vb5)), (f64(vw7), f64(vb7))])
    return q, k, v

@@ -1,0 +1,259 @@
+from contextlib import ExitStack
+
+import concourse.mybir as mybir
+from concourse.masks import make_identity
+
+F32 = mybir.dt.float32
+BF16 = mybir.dt.bfloat16
+U32 = mybir.dt.uint32
+U8 = mybir.dt.uint8
+FP8X4 = mybir.dt.float8_e4m3fn_x4
+ALU = mybir.AluOpType
+ACT = mybir.ActivationFunctionType
+
+BATCH = 2
+SEQ = 2048
+EMBED = 512
+PROJ = 3
+GROUPS = 4
+HEADS_IN_GROUP = 2
+HEAD_DIM = 64
+
+P = 128
+PACK = 4
+BLOCKS = SEQ // P
+BANK_BLOCKS = 4
+BANKS = BLOCKS // BANK_BLOCKS
+PADDED = P + 1
+X_COLS = BLOCKS * PADDED
+SLOT = 16
+X_BUFFERS = 3
+
+FLOPS = 2 * BATCH * SEQ * EMBED * PROJ * EMBED + 2 * BATCH * SEQ * PROJ * P * (3 + 5 + 7)
+
+
+def tile_tranceptionblockattention_pa_t_kernel(
+    tc, hidden_states, c_attn_w, c_attn_b,
+    qw3, qb3, qw5, qb5, qw7, qb7,
+    kw3, kb3, kw5, kb5, kw7, kb7,
+    vw3, vb3, vw5, vb5, vw7, vb7,
+    out_0, out_1, out_2,
+):
+    nc = tc.nc
+    conv_w = [[qw3, qw5, qw7], [kw3, kw5, kw7], [vw3, vw5, vw7]]
+    conv_b = [[qb3, qb5, qb7], [kb3, kb5, kb7], [vb3, vb5, vb7]]
+    outs = [out_0, out_1, out_2]
+
+    with ExitStack() as stack:
+        keep = stack.enter_context(tc.tile_pool(name="keep", bufs=1))
+        x_in = stack.enter_context(tc.tile_pool(name="x_in", bufs=4))
+        stage = stack.enter_context(tc.tile_pool(name="stage", bufs=2))
+        seeds = stack.enter_context(tc.tile_pool(name="seeds", bufs=3))
+        terms = stack.enter_context(tc.tile_pool(name="terms", bufs=8))
+        results = stack.enter_context(tc.tile_pool(name="results", bufs=3))
+        feat_psum = stack.enter_context(tc.psum_pool(name="feat_psum", bufs=4))
+        tok_psum = stack.enter_context(tc.psum_pool(name="tok_psum", bufs=4))
+
+        ident = keep.tile([P, P], F32)
+        make_identity(nc, ident[:])
+
+        w_raw = keep.tile([P, PACK, PROJ * EMBED], BF16)
+        nc.scalar.dma_start(
+            out=w_raw[:].rearrange("q (u e) c -> q u (e c)", u=2),
+            in_=c_attn_w.rearrange("(u q e) c -> q u (e c)", u=2, e=2),
+        )
+        w_codes = keep.tile([P, PROJ * EMBED], U32, align_bytes=64)
+        w_scales = keep.tile([P, PROJ * EMBED], U8, align_bytes=64)
+        for proj in range(PROJ):
+            cols = slice(proj * EMBED, (proj + 1) * EMBED)
+            w_grouped = stage.tile([P, EMBED, PACK], BF16, align_bytes=64)
+            nc.vector.tensor_copy(out=w_grouped[:], in_=w_raw[:, :, cols].rearrange("q j c -> q c j"))
+            nc.vector.quantize_mx(
+                out=w_codes[:, cols].bitcast(FP8X4),
+                scales=w_scales[:, cols],
+                in_=w_grouped[:].rearrange("q c j -> q (c j)"),
+            )
+
+        x_codes = keep.tile([P, BATCH * SEQ], U32, align_bytes=64)
+        x_scales = keep.tile([P, BATCH * SEQ], U8, align_bytes=64)
+        x_view = hidden_states.rearrange("b (p t) k -> b p t k", t=BLOCKS)
+
+        def quantise_batch(b):
+            for bank in range(BANKS):
+                first = bank * BANK_BLOCKS
+                x_raw = x_in.tile([P, BANK_BLOCKS, EMBED], BF16)
+                nc.sync.dma_start(out=x_raw[:], in_=x_view[b, :, first : first + BANK_BLOCKS, :])
+                x_words = x_raw[:].bitcast(F32)
+                x_grouped = stage.tile([P, BANK_BLOCKS * P, PACK], BF16, align_bytes=64)
+                grouped_words = x_grouped[:].bitcast(F32)
+                for half in range(2):
+                    turned = tok_psum.tile([P, 2, 2, P], F32, tag="tok")
+                    for i in range(2):
+                        for u in range(2):
+                            nc.tensor.transpose(
+                                turned[:, i, u, :], x_words[:, 2 * half + i, u * P : (u + 1) * P], ident[:]
+                            )
+                    nc.scalar.copy(
+                        out=grouped_words[:, half * 2 * P : (half + 1) * 2 * P, :].rearrange(
+                            "q (i p) u -> q i p u", i=2
+                        ),
+                        in_=turned[:].rearrange("q i u p -> q i p u"),
+                    )
+                cols = slice(b * SEQ + first * P, b * SEQ + (first + BANK_BLOCKS) * P)
+                nc.vector.quantize_mx(
+                    out=x_codes[:, cols].bitcast(FP8X4),
+                    scales=x_scales[:, cols],
+                    in_=x_grouped[:].rearrange("q c j -> q (c j)"),
+                )
+
+        quantise_batch(0)
+
+        bias_rows = keep.tile([P, PROJ, P], BF16)
+        for proj in range(PROJ):
+            nc.sync.dma_start(
+                out=bias_rows[:, proj, :],
+                in_=c_attn_b[proj * EMBED : proj * EMBED + P].partition_broadcast(P),
+            )
+        bias_cols = keep.tile([P, PROJ, SLOT], BF16)
+        with nc.allow_non_contiguous_dma(reason="one bias value per partition"):
+            for proj in range(PROJ):
+                nc.sync.dma_start(
+                    out=bias_cols[:, proj, 1:GROUPS],
+                    in_=c_attn_b[proj * EMBED + P : (proj + 1) * EMBED].rearrange("(g f) -> f g", f=P),
+                )
+        tap_w = keep.tile([P, PROJ, GROUPS, SLOT], BF16)
+        tap_b = keep.tile([P, PROJ, GROUPS, SLOT], BF16)
+        seed_w = keep.tile([P, PROJ, GROUPS], F32)
+        for proj in range(PROJ):
+            for g in range(1, GROUPS):
+                taps = 2 * g + 1
+                for head in range(HEADS_IN_GROUP):
+                    rows = slice(head * HEAD_DIM, (head + 1) * HEAD_DIM)
+                    nc.sync.dma_start(out=tap_w[rows, proj, g, 0:taps], in_=conv_w[proj][g - 1])
+                    nc.sync.dma_start(
+                        out=tap_b[rows, proj, g, 0:1],
+                        in_=conv_b[proj][g - 1].rearrange("(d o) -> d o", o=1),
+                    )
+                nc.vector.tensor_copy(out=seed_w[:, proj, g : g + 1], in_=tap_w[:, proj, g, taps - 1 : taps])
+
+        x_tiles = [keep.tile([P, X_COLS], F32, name="x_tile%d" % n) for n in range(X_BUFFERS)]
+        for x_tile in x_tiles:
+            nc.vector.memset(x_tile[:].rearrange("f (t c) -> f t c", c=PADDED)[:, :, 0:1], 0.0)
+
+        def store(b, proj, g, result):
+            heads = slice(g * HEADS_IN_GROUP, (g + 1) * HEADS_IN_GROUP)
+            nc.sync.dma_start(
+                out=outs[proj][b, heads, :, :].rearrange("h (p t) d -> p h (t d)", t=BLOCKS),
+                in_=result[:].rearrange("p h t d -> p h (t d)"),
+            )
+
+        def plain_group(b, proj):
+            result = results.tile([P, HEADS_IN_GROUP, BLOCKS, HEAD_DIM], F32)
+            w_cols = slice(proj * EMBED, proj * EMBED + P)
+            for bank in range(BANKS):
+                first = bank * BANK_BLOCKS
+                by_token = tok_psum.tile([P, BANK_BLOCKS, P], F32, tag="tok")
+                for i in range(BANK_BLOCKS):
+                    x_cols = slice(b * SEQ + (first + i) * P, b * SEQ + (first + i + 1) * P)
+                    nc.tensor.matmul_mx(
+                        out=by_token[:, i, :],
+                        lhsT=x_codes[:, x_cols].bitcast(FP8X4),
+                        lhsT_scale=x_scales[:, x_cols],
+                        rhs=w_codes[:, w_cols].bitcast(FP8X4),
+                        rhs_scale=w_scales[:, w_cols],
+                        start=True,
+                        stop=True,
+                    )
+                nc.vector.tensor_tensor(
+                    out=result[:, :, first : first + BANK_BLOCKS, :],
+                    in0=by_token[:].rearrange("p t (h d) -> p h t d", h=HEADS_IN_GROUP),
+                    in1=bias_rows[:, proj, :]
+                    .rearrange("p (h d) -> p h d", h=HEADS_IN_GROUP)
+                    .unsqueeze(2)
+                    .to_broadcast([P, HEADS_IN_GROUP, BANK_BLOCKS, HEAD_DIM]),
+                    op=ALU.add,
+                )
+            store(b, proj, 0, result)
+
+        def conv_group(b, proj, g, x_tile):
+            taps = 2 * g + 1
+            w_cols = slice(proj * EMBED + g * P, proj * EMBED + (g + 1) * P)
+
+            def weight(back):
+                return tap_w[:, proj, g, taps - 1 - back : taps - back]
+
+            x_blocks = x_tile[:].rearrange("f (t c) -> f t c", c=PADDED)
+            for bank in range(BANKS):
+                first = bank * BANK_BLOCKS
+                x_cols = slice(b * SEQ + first * P, b * SEQ + (first + BANK_BLOCKS) * P)
+                by_feature = feat_psum.tile([P, BANK_BLOCKS, P], F32)
+                nc.tensor.matmul_mx(
+                    out=by_feature[:].rearrange("f t p -> f (t p)"),
+                    lhsT=w_codes[:, w_cols].bitcast(FP8X4),
+                    lhsT_scale=w_scales[:, w_cols],
+                    rhs=x_codes[:, x_cols].bitcast(FP8X4),
+                    rhs_scale=x_scales[:, x_cols],
+                    start=True,
+                    stop=True,
+                )
+                nc.scalar.activation(
+                    out=x_blocks[:, first : first + BANK_BLOCKS, 1:PADDED],
+                    in_=by_feature[:],
+                    func=ACT.Identity,
+                    bias=bias_cols[:, proj, g : g + 1],
+                    scale=1.0,
+                )
+
+            seed = seeds.tile([P, X_COLS], F32)
+            nc.scalar.activation(
+                out=seed[:], in_=x_tile[:], func=ACT.Identity,
+                scale=seed_w[:, proj, g : g + 1], bias=tap_b[:, proj, g, 0:1],
+            )
+            nc.vector.scalar_tensor_tensor(
+                out=seed[:, PADDED:X_COLS], in0=x_tile[:, 0 : X_COLS - PADDED], scalar=weight(1),
+                in1=seed[:, PADDED:X_COLS], op0=ALU.mult, op1=ALU.add,
+            )
+            nc.vector.scalar_tensor_tensor(
+                out=seed[:, 1:PADDED], in0=x_tile[:, X_COLS - PADDED : X_COLS - 1], scalar=weight(1),
+                in1=seed[:, 1:PADDED], op0=ALU.mult, op1=ALU.add,
+            )
+            shifted_terms = [(seed, 0)]
+            for back in range(2, taps):
+                term = terms.tile([P, X_COLS], F32)
+                nc.vector.tensor_scalar_mul(out=term[:], in0=x_tile[:], scalar1=weight(back))
+                shifted_terms.append((term, back))
+
+            result = results.tile([P, HEADS_IN_GROUP, BLOCKS, HEAD_DIM], F32)
+            for bank in range(BANKS):
+                first = bank * BANK_BLOCKS
+                by_token = tok_psum.tile([P, BANK_BLOCKS, P], F32, tag="tok")
+                for i in range(BANK_BLOCKS):
+                    for n, (term, back) in enumerate(shifted_terms):
+                        block = first + i - back
+                        if block >= 0:
+                            start_col = block * PADDED + 1
+                        else:
+                            start_col = (block + BLOCKS) * PADDED
+                        nc.tensor.matmul(
+                            out=by_token[:, i, :],
+                            lhsT=term[:, start_col : start_col + P],
+                            rhs=ident[:],
+                            is_transpose=True,
+                            start=(n == 0),
+                            stop=(n == len(shifted_terms) - 1),
+                        )
+                nc.scalar.copy(
+                    out=result[:, :, first : first + BANK_BLOCKS, :],
+                    in_=by_token[:].rearrange("p t (h d) -> p h t d", h=HEADS_IN_GROUP),
+                )
+            store(b, proj, g, result)
+
+        conv_groups_done = 0
+        for b in range(BATCH):
+            for proj in range(PROJ):
+                plain_group(b, proj)
+                for g in range(1, GROUPS):
+                    conv_group(b, proj, g, x_tiles[conv_groups_done % X_BUFFERS])
+                    conv_groups_done += 1
+                if proj == 0 and b + 1 < BATCH:
+                    quantise_batch(b + 1)

@@ -28,6 +28,7 @@ PADDED = P + 1
 X_COLS = BLOCKS * PADDED
 SLOT = 16
 X_BUFFERS = 3
+MAX_TERMS = 2
 
 FLOPS = 2 * BATCH * SEQ * EMBED * PROJ * EMBED + 2 * BATCH * SEQ * PROJ * P * (3 + 5 + 7)
 
@@ -48,8 +49,7 @@ def tile_tranceptionblockattention_pa_t_kernel(
         keep = stack.enter_context(tc.tile_pool(name="keep", bufs=1))
         x_in = stack.enter_context(tc.tile_pool(name="x_in", bufs=4))
         stage = stack.enter_context(tc.tile_pool(name="stage", bufs=2))
-        seeds = stack.enter_context(tc.tile_pool(name="seeds", bufs=3))
-        terms = stack.enter_context(tc.tile_pool(name="terms", bufs=8))
+        terms = stack.enter_context(tc.tile_pool(name="terms", bufs=6))
         results = stack.enter_context(tc.tile_pool(name="results", bufs=3))
         feat_psum = stack.enter_context(tc.psum_pool(name="feat_psum", bufs=4))
         tok_psum = stack.enter_context(tc.psum_pool(name="tok_psum", bufs=4))
@@ -121,20 +121,20 @@ def tile_tranceptionblockattention_pa_t_kernel(
                     out=bias_cols[:, proj, 1:GROUPS],
                     in_=c_attn_b[proj * EMBED + P : (proj + 1) * EMBED].rearrange("(g f) -> f g", f=P),
                 )
-        tap_w = keep.tile([P, PROJ, GROUPS, SLOT], BF16)
+        tap_w_bf = keep.tile([P, PROJ, GROUPS, SLOT], BF16)
         tap_b = keep.tile([P, PROJ, GROUPS, SLOT], BF16)
-        seed_w = keep.tile([P, PROJ, GROUPS], F32)
+        tap_w = keep.tile([P, PROJ, GROUPS, SLOT], F32)
         for proj in range(PROJ):
             for g in range(1, GROUPS):
                 taps = 2 * g + 1
                 for head in range(HEADS_IN_GROUP):
                     rows = slice(head * HEAD_DIM, (head + 1) * HEAD_DIM)
-                    nc.sync.dma_start(out=tap_w[rows, proj, g, 0:taps], in_=conv_w[proj][g - 1])
+                    nc.sync.dma_start(out=tap_w_bf[rows, proj, g, 0:taps], in_=conv_w[proj][g - 1])
                     nc.sync.dma_start(
                         out=tap_b[rows, proj, g, 0:1],
                         in_=conv_b[proj][g - 1].rearrange("(d o) -> d o", o=1),
                     )
-                nc.vector.tensor_copy(out=seed_w[:, proj, g : g + 1], in_=tap_w[:, proj, g, taps - 1 : taps])
+                nc.vector.tensor_copy(out=tap_w[:, proj, g, 0:taps], in_=tap_w_bf[:, proj, g, 0:taps])
 
         x_tiles = [keep.tile([P, X_COLS], F32, name="x_tile%d" % n) for n in range(X_BUFFERS)]
         for x_tile in x_tiles:
@@ -204,24 +204,31 @@ def tile_tranceptionblockattention_pa_t_kernel(
                     scale=1.0,
                 )
 
-            seed = seeds.tile([P, X_COLS], F32)
-            nc.scalar.activation(
-                out=seed[:], in_=x_tile[:], func=ACT.Identity,
-                scale=seed_w[:, proj, g : g + 1], bias=tap_b[:, proj, g, 0:1],
-            )
-            nc.vector.scalar_tensor_tensor(
-                out=seed[:, PADDED:X_COLS], in0=x_tile[:, 0 : X_COLS - PADDED], scalar=weight(1),
-                in1=seed[:, PADDED:X_COLS], op0=ALU.mult, op1=ALU.add,
-            )
-            nc.vector.scalar_tensor_tensor(
-                out=seed[:, 1:PADDED], in0=x_tile[:, X_COLS - PADDED : X_COLS - 1], scalar=weight(1),
-                in1=seed[:, 1:PADDED], op0=ALU.mult, op1=ALU.add,
-            )
-            shifted_terms = [(seed, 0)]
-            for back in range(2, taps):
+            n_terms = min(g, MAX_TERMS)
+            term_taps = -(-taps // n_terms)
+            shifted_terms = []
+            for first_back in range(0, taps, term_taps):
                 term = terms.tile([P, X_COLS], F32)
-                nc.vector.tensor_scalar_mul(out=term[:], in0=x_tile[:], scalar1=weight(back))
-                shifted_terms.append((term, back))
+                nc.scalar.activation(
+                    out=term[:], in_=x_tile[:], func=ACT.Identity, scale=weight(first_back),
+                    bias=(tap_b[:, proj, g, 0:1] if first_back == 0 else 0.0),
+                )
+                shifted_terms.append((term, first_back))
+            for further in range(1, term_taps):
+                growing = [(term, first_back) for term, first_back in shifted_terms if first_back + further < taps]
+                for term, first_back in growing:
+                    nc.vector.scalar_tensor_tensor(
+                        out=term[:, further * PADDED : X_COLS], in0=x_tile[:, 0 : X_COLS - further * PADDED],
+                        scalar=weight(first_back + further), in1=term[:, further * PADDED : X_COLS],
+                        op0=ALU.mult, op1=ALU.add,
+                    )
+                for term, first_back in growing:
+                    term_blocks = term[:].rearrange("f (t c) -> f t c", c=PADDED)
+                    nc.vector.scalar_tensor_tensor(
+                        out=term_blocks[:, 0:further, 1:PADDED], in0=x_blocks[:, BLOCKS - further : BLOCKS, 0:P],
+                        scalar=weight(first_back + further), in1=term_blocks[:, 0:further, 1:PADDED],
+                        op0=ALU.mult, op1=ALU.add,
+                    )
 
             result = results.tile([P, HEADS_IN_GROUP, BLOCKS, HEAD_DIM], F32)
             for bank in range(BANKS):
@@ -250,10 +257,13 @@ def tile_tranceptionblockattention_pa_t_kernel(
 
         conv_groups_done = 0
         for b in range(BATCH):
+            group_order = list(range(GROUPS)) if b == 0 else list(reversed(range(GROUPS)))
             for proj in range(PROJ):
-                plain_group(b, proj)
-                for g in range(1, GROUPS):
-                    conv_group(b, proj, g, x_tiles[conv_groups_done % X_BUFFERS])
-                    conv_groups_done += 1
+                for g in group_order:
+                    if g == 0:
+                        plain_group(b, proj)
+                    else:
+                        conv_group(b, proj, g, x_tiles[conv_groups_done % X_BUFFERS])
+                        conv_groups_done += 1
                 if proj == 0 and b + 1 < BATCH:
                     quantise_batch(b + 1)

@@ -27,8 +27,9 @@ BANKS = BLOCKS // BANK_BLOCKS
 PADDED = P + 1
 X_COLS = BLOCKS * PADDED
 SLOT = 16
-X_BUFFERS = 3
+X_BUFFERS = 4
 MAX_TERMS = 2
+TENSOR_TAP_BLOCKS = 8
 
 FLOPS = 2 * BATCH * SEQ * EMBED * PROJ * EMBED + 2 * BATCH * SEQ * PROJ * P * (3 + 5 + 7)
 
@@ -47,7 +48,7 @@ def tile_tranceptionblockattention_pa_t_kernel(
 
     with ExitStack() as stack:
         keep = stack.enter_context(tc.tile_pool(name="keep", bufs=1))
-        x_in = stack.enter_context(tc.tile_pool(name="x_in", bufs=4))
+        x_in = stack.enter_context(tc.tile_pool(name="x_in", bufs=BANKS))
         stage = stack.enter_context(tc.tile_pool(name="stage", bufs=2))
         terms = stack.enter_context(tc.tile_pool(name="terms", bufs=6))
         results = stack.enter_context(tc.tile_pool(name="results", bufs=3))
@@ -58,13 +59,18 @@ def tile_tranceptionblockattention_pa_t_kernel(
         make_identity(nc, ident[:])
 
         w_raw = keep.tile([P, PACK, PROJ * EMBED], BF16)
-        nc.scalar.dma_start(
-            out=w_raw[:].rearrange("q (u e) c -> q u (e c)", u=2),
-            in_=c_attn_w.rearrange("(u q e) c -> q u (e c)", u=2, e=2),
-        )
         w_codes = keep.tile([P, PROJ * EMBED], U32, align_bytes=64)
         w_scales = keep.tile([P, PROJ * EMBED], U8, align_bytes=64)
-        for proj in range(PROJ):
+
+        def load_weights(proj):
+            cols = slice(proj * EMBED, (proj + 1) * EMBED)
+            for u in range(2):
+                nc.sync.dma_start(
+                    out=w_raw[:, 2 * u : 2 * u + 2, cols],
+                    in_=c_attn_w[u * 2 * P : (u + 1) * 2 * P, cols].rearrange("(q e) c -> q e c", e=2),
+                )
+
+        def quantise_weights(proj):
             cols = slice(proj * EMBED, (proj + 1) * EMBED)
             w_grouped = stage.tile([P, EMBED, PACK], BF16, align_bytes=64)
             nc.vector.tensor_copy(out=w_grouped[:], in_=w_raw[:, :, cols].rearrange("q j c -> q c j"))
@@ -78,11 +84,19 @@ def tile_tranceptionblockattention_pa_t_kernel(
         x_scales = keep.tile([P, BATCH * SEQ], U8, align_bytes=64)
         x_view = hidden_states.rearrange("b (p t) k -> b p t k", t=BLOCKS)
 
-        def quantise_batch(b):
+        def load_batch(b):
+            loaded = []
             for bank in range(BANKS):
                 first = bank * BANK_BLOCKS
                 x_raw = x_in.tile([P, BANK_BLOCKS, EMBED], BF16)
                 nc.sync.dma_start(out=x_raw[:], in_=x_view[b, :, first : first + BANK_BLOCKS, :])
+                loaded.append(x_raw)
+            return loaded
+
+        def quantise_batch(b, loaded):
+            for bank in range(BANKS):
+                first = bank * BANK_BLOCKS
+                x_raw = loaded[bank]
                 x_words = x_raw[:].bitcast(F32)
                 x_grouped = stage.tile([P, BANK_BLOCKS * P, PACK], BF16, align_bytes=64)
                 grouped_words = x_grouped[:].bitcast(F32)
@@ -106,26 +120,28 @@ def tile_tranceptionblockattention_pa_t_kernel(
                     in_=x_grouped[:].rearrange("q c j -> q (c j)"),
                 )
 
-        quantise_batch(0)
-
         bias_rows = keep.tile([P, PROJ, P], BF16)
-        for proj in range(PROJ):
-            nc.sync.dma_start(
-                out=bias_rows[:, proj, :],
-                in_=c_attn_b[proj * EMBED : proj * EMBED + P].partition_broadcast(P),
-            )
         bias_cols = keep.tile([P, PROJ, SLOT], BF16)
-        with nc.allow_non_contiguous_dma(reason="one bias value per partition"):
-            for proj in range(PROJ):
-                nc.sync.dma_start(
-                    out=bias_cols[:, proj, 1:GROUPS],
-                    in_=c_attn_b[proj * EMBED + P : (proj + 1) * EMBED].rearrange("(g f) -> f g", f=P),
-                )
         tap_w_bf = keep.tile([P, PROJ, GROUPS, SLOT], BF16)
         tap_b = keep.tile([P, PROJ, GROUPS, SLOT], BF16)
         tap_w = keep.tile([P, PROJ, GROUPS, SLOT], F32)
-        for proj in range(PROJ):
-            for g in range(1, GROUPS):
+        furthest_diag = keep.tile([P, PROJ, GROUPS, P], F32)
+
+        def load_biases():
+            for proj in range(PROJ):
+                nc.sync.dma_start(
+                    out=bias_rows[:, proj, :],
+                    in_=c_attn_b[proj * EMBED : proj * EMBED + P].partition_broadcast(P),
+                )
+            with nc.allow_non_contiguous_dma(reason="one bias value per partition"):
+                for proj in range(PROJ):
+                    nc.sync.dma_start(
+                        out=bias_cols[:, proj, 1:GROUPS],
+                        in_=c_attn_b[proj * EMBED + P : (proj + 1) * EMBED].rearrange("(g f) -> f g", f=P),
+                    )
+
+        def load_taps(proj):
+            for g in reversed(range(1, GROUPS)):
                 taps = 2 * g + 1
                 for head in range(HEADS_IN_GROUP):
                     rows = slice(head * HEAD_DIM, (head + 1) * HEAD_DIM)
@@ -135,6 +151,22 @@ def tile_tranceptionblockattention_pa_t_kernel(
                         in_=conv_b[proj][g - 1].rearrange("(d o) -> d o", o=1),
                     )
                 nc.vector.tensor_copy(out=tap_w[:, proj, g, 0:taps], in_=tap_w_bf[:, proj, g, 0:taps])
+                nc.vector.tensor_scalar_mul(
+                    out=furthest_diag[:, proj, g, :], in0=ident[:], scalar1=tap_w[:, proj, g, 0:1]
+                )
+
+        load_weights(0)
+        first_batch = load_batch(0)
+        load_biases()
+        load_taps(0)
+        for proj in range(1, PROJ):
+            load_weights(proj)
+        for proj in range(1, PROJ):
+            load_taps(proj)
+        quantise_weights(0)
+        quantise_batch(0, first_batch)
+        for proj in range(1, PROJ):
+            quantise_weights(proj)
 
         x_tiles = [keep.tile([P, X_COLS], F32, name="x_tile%d" % n) for n in range(X_BUFFERS)]
         for x_tile in x_tiles:
@@ -209,44 +241,69 @@ def tile_tranceptionblockattention_pa_t_kernel(
             shifted_terms = []
             for first_back in range(0, taps, term_taps):
                 term = terms.tile([P, X_COLS], F32)
-                nc.scalar.activation(
-                    out=term[:], in_=x_tile[:], func=ACT.Identity, scale=weight(first_back),
-                    bias=(tap_b[:, proj, g, 0:1] if first_back == 0 else 0.0),
-                )
+                if first_back > 0 and g == 2:
+                    nc.vector.tensor_scalar_mul(out=term[:], in0=x_tile[:], scalar1=weight(first_back))
+                else:
+                    nc.scalar.activation(
+                        out=term[:], in_=x_tile[:], func=ACT.Identity, scale=weight(first_back),
+                        bias=(tap_b[:, proj, g, 0:1] if first_back == 0 else 0.0),
+                    )
                 shifted_terms.append((term, first_back))
             for further in range(1, term_taps):
                 growing = [(term, first_back) for term, first_back in shifted_terms if first_back + further < taps]
                 for term, first_back in growing:
-                    nc.vector.scalar_tensor_tensor(
-                        out=term[:, further * PADDED : X_COLS], in0=x_tile[:, 0 : X_COLS - further * PADDED],
-                        scalar=weight(first_back + further), in1=term[:, further * PADDED : X_COLS],
-                        op0=ALU.mult, op1=ALU.add,
-                    )
+                    back = first_back + further
+                    if back == taps - 1:
+                        nc.vector.scalar_tensor_tensor(
+                            out=term[:, (TENSOR_TAP_BLOCKS - first_back) * PADDED : (BLOCKS - first_back) * PADDED],
+                            in0=x_tile[:, (TENSOR_TAP_BLOCKS - back) * PADDED : (BLOCKS - back) * PADDED],
+                            scalar=weight(back),
+                            in1=term[:, (TENSOR_TAP_BLOCKS - first_back) * PADDED : (BLOCKS - first_back) * PADDED],
+                            op0=ALU.mult, op1=ALU.add,
+                        )
+                    else:
+                        nc.vector.scalar_tensor_tensor(
+                            out=term[:, further * PADDED : X_COLS], in0=x_tile[:, 0 : X_COLS - further * PADDED],
+                            scalar=weight(back), in1=term[:, further * PADDED : X_COLS],
+                            op0=ALU.mult, op1=ALU.add,
+                        )
                 for term, first_back in growing:
-                    term_blocks = term[:].rearrange("f (t c) -> f t c", c=PADDED)
-                    nc.vector.scalar_tensor_tensor(
-                        out=term_blocks[:, 0:further, 1:PADDED], in0=x_blocks[:, BLOCKS - further : BLOCKS, 0:P],
-                        scalar=weight(first_back + further), in1=term_blocks[:, 0:further, 1:PADDED],
-                        op0=ALU.mult, op1=ALU.add,
-                    )
+                    back = first_back + further
+                    if back < taps - 1:
+                        term_blocks = term[:].rearrange("f (t c) -> f t c", c=PADDED)
+                        nc.vector.scalar_tensor_tensor(
+                            out=term_blocks[:, 0:further, 1:PADDED], in0=x_blocks[:, BLOCKS - further : BLOCKS, 0:P],
+                            scalar=weight(back), in1=term_blocks[:, 0:further, 1:PADDED],
+                            op0=ALU.mult, op1=ALU.add,
+                        )
+
+            def block_from(back, t):
+                block = t - back
+                if block >= 0:
+                    return slice(block * PADDED + 1, block * PADDED + 1 + P)
+                return slice((block + BLOCKS) * PADDED, (block + BLOCKS) * PADDED + P)
 
             result = results.tile([P, HEADS_IN_GROUP, BLOCKS, HEAD_DIM], F32)
             for bank in range(BANKS):
                 first = bank * BANK_BLOCKS
                 by_token = tok_psum.tile([P, BANK_BLOCKS, P], F32, tag="tok")
                 for i in range(BANK_BLOCKS):
-                    for n, (term, back) in enumerate(shifted_terms):
-                        block = first + i - back
-                        if block >= 0:
-                            start_col = block * PADDED + 1
-                        else:
-                            start_col = (block + BLOCKS) * PADDED
+                    t = first + i
+                    if t < TENSOR_TAP_BLOCKS:
                         nc.tensor.matmul(
                             out=by_token[:, i, :],
-                            lhsT=term[:, start_col : start_col + P],
+                            lhsT=x_tile[:, block_from(taps - 1, t)],
+                            rhs=furthest_diag[:, proj, g, :],
+                            start=True,
+                            stop=False,
+                        )
+                    for n, (term, first_back) in enumerate(shifted_terms):
+                        nc.tensor.matmul(
+                            out=by_token[:, i, :],
+                            lhsT=term[:, block_from(first_back, t)],
                             rhs=ident[:],
                             is_transpose=True,
-                            start=(n == 0),
+                            start=(n == 0 and t >= TENSOR_TAP_BLOCKS),
                             stop=(n == len(shifted_terms) - 1),
                         )
                 nc.scalar.copy(
@@ -257,13 +314,15 @@ def tile_tranceptionblockattention_pa_t_kernel(
 
         conv_groups_done = 0
         for b in range(BATCH):
-            group_order = list(range(GROUPS)) if b == 0 else list(reversed(range(GROUPS)))
+            if b == 0:
+                for proj in range(PROJ):
+                    plain_group(b, proj)
             for proj in range(PROJ):
-                for g in group_order:
-                    if g == 0:
-                        plain_group(b, proj)
-                    else:
-                        conv_group(b, proj, g, x_tiles[conv_groups_done % X_BUFFERS])
-                        conv_groups_done += 1
+                for g in reversed(range(1, GROUPS)):
+                    conv_group(b, proj, g, x_tiles[conv_groups_done % X_BUFFERS])
+                    conv_groups_done += 1
                 if proj == 0 and b + 1 < BATCH:
-                    quantise_batch(b + 1)
+                    quantise_batch(b + 1, load_batch(b + 1))
+            if b == BATCH - 1:
+                for proj in range(PROJ):
+                    plain_group(b, proj)

@@ -26,10 +26,17 @@ BANK_BLOCKS = 4
 BANKS = BLOCKS // BANK_BLOCKS
 PADDED = P + 1
 X_COLS = BLOCKS * PADDED
+BANK_COLS = BANK_BLOCKS * PADDED
 SLOT = 16
-X_BUFFERS = 4
-MAX_TERMS = 2
-TENSOR_TAP_BLOCKS = 8
+TERM_TAPS = 2
+TENSOR_EVERY = 4
+MX_RUN = 2
+X_AHEAD = 3
+FIRST_TERM_AHEAD = 2
+X_TILES = X_AHEAD + 2
+GROUP_ORDER = [[1, 2, 3], [3, 2, 1]]
+TURN_FROM_ROUND = 1
+assert X_AHEAD == PROJ
 
 FLOPS = 2 * BATCH * SEQ * EMBED * PROJ * EMBED + 2 * BATCH * SEQ * PROJ * P * (3 + 5 + 7)
 
@@ -50,10 +57,12 @@ def tile_tranceptionblockattention_pa_t_kernel(
         keep = stack.enter_context(tc.tile_pool(name="keep", bufs=1))
         x_in = stack.enter_context(tc.tile_pool(name="x_in", bufs=BANKS))
         stage = stack.enter_context(tc.tile_pool(name="stage", bufs=2))
-        terms = stack.enter_context(tc.tile_pool(name="terms", bufs=6))
-        results = stack.enter_context(tc.tile_pool(name="results", bufs=3))
-        feat_psum = stack.enter_context(tc.psum_pool(name="feat_psum", bufs=4))
-        tok_psum = stack.enter_context(tc.psum_pool(name="tok_psum", bufs=4))
+        first_terms = stack.enter_context(tc.tile_pool(name="first_terms", bufs=FIRST_TERM_AHEAD + 2))
+        other_terms = stack.enter_context(tc.tile_pool(name="other_terms", bufs=6))
+        results = stack.enter_context(tc.tile_pool(name="results", bufs=2 * BANKS))
+        project_psum = stack.enter_context(tc.psum_pool(name="project_psum", bufs=BANKS))
+        turn_psum = stack.enter_context(tc.psum_pool(name="turn_psum", bufs=BANKS))
+        stack.enter_context(tc.manual_schedule())
 
         ident = keep.tile([P, P], F32)
         make_identity(nc, ident[:])
@@ -85,119 +94,125 @@ def tile_tranceptionblockattention_pa_t_kernel(
         x_view = hidden_states.rearrange("b (p t) k -> b p t k", t=BLOCKS)
 
         def load_batch(b):
-            loaded = []
+            quarters = []
             for bank in range(BANKS):
                 first = bank * BANK_BLOCKS
                 x_raw = x_in.tile([P, BANK_BLOCKS, EMBED], BF16)
                 nc.sync.dma_start(out=x_raw[:], in_=x_view[b, :, first : first + BANK_BLOCKS, :])
-                loaded.append(x_raw)
-            return loaded
+                quarters.append(x_raw)
+            return quarters
 
-        def quantise_batch(b, loaded):
-            for bank in range(BANKS):
-                first = bank * BANK_BLOCKS
-                x_raw = loaded[bank]
-                x_words = x_raw[:].bitcast(F32)
-                x_grouped = stage.tile([P, BANK_BLOCKS * P, PACK], BF16, align_bytes=64)
-                grouped_words = x_grouped[:].bitcast(F32)
-                for half in range(2):
-                    turned = tok_psum.tile([P, 2, 2, P], F32, tag="tok")
-                    for i in range(2):
-                        for u in range(2):
-                            nc.tensor.transpose(
-                                turned[:, i, u, :], x_words[:, 2 * half + i, u * P : (u + 1) * P], ident[:]
-                            )
-                    nc.scalar.copy(
-                        out=grouped_words[:, half * 2 * P : (half + 1) * 2 * P, :].rearrange(
-                            "q (i p) u -> q i p u", i=2
-                        ),
-                        in_=turned[:].rearrange("q i u p -> q i p u"),
-                    )
-                cols = slice(b * SEQ + first * P, b * SEQ + (first + BANK_BLOCKS) * P)
-                nc.vector.quantize_mx(
-                    out=x_codes[:, cols].bitcast(FP8X4),
-                    scales=x_scales[:, cols],
-                    in_=x_grouped[:].rearrange("q c j -> q (c j)"),
+        def turn_quarter(x_raw):
+            x_words = x_raw[:].bitcast(F32)
+            x_grouped = stage.tile([P, BANK_BLOCKS * P, PACK], BF16, align_bytes=64, bufs=BANKS)
+            grouped_words = x_grouped[:].bitcast(F32)
+            for half in range(2):
+                turned = turn_psum.tile([P, 2, 2, P], F32, tag="turn")
+                for i in range(2):
+                    for u in range(2):
+                        nc.tensor.transpose(
+                            turned[:, i, u, :], x_words[:, 2 * half + i, u * P : (u + 1) * P], ident[:]
+                        )
+                nc.scalar.copy(
+                    out=grouped_words[:, half * 2 * P : (half + 1) * 2 * P, :].rearrange(
+                        "q (i p) u -> q i p u", i=2
+                    ),
+                    in_=turned[:].rearrange("q i u p -> q i p u"),
                 )
+            return x_grouped
+
+        def quantise_quarter(b, bank, x_grouped):
+            cols = slice(b * SEQ + bank * BANK_BLOCKS * P, b * SEQ + (bank + 1) * BANK_BLOCKS * P)
+            nc.vector.quantize_mx(
+                out=x_codes[:, cols].bitcast(FP8X4),
+                scales=x_scales[:, cols],
+                in_=x_grouped[:].rearrange("q c j -> q (c j)"),
+            )
 
         bias_rows = keep.tile([P, PROJ, P], BF16)
         bias_cols = keep.tile([P, PROJ, SLOT], BF16)
         tap_w_bf = keep.tile([P, PROJ, GROUPS, SLOT], BF16)
         tap_b = keep.tile([P, PROJ, GROUPS, SLOT], BF16)
         tap_w = keep.tile([P, PROJ, GROUPS, SLOT], F32)
-        furthest_diag = keep.tile([P, PROJ, GROUPS, P], F32)
+        last_diag = keep.tile([P, PROJ, GROUPS, P], F32)
 
-        def load_biases():
-            for proj in range(PROJ):
-                nc.sync.dma_start(
-                    out=bias_rows[:, proj, :],
-                    in_=c_attn_b[proj * EMBED : proj * EMBED + P].partition_broadcast(P),
-                )
+        def load_biases(proj):
+            nc.sync.dma_start(
+                out=bias_rows[:, proj, :],
+                in_=c_attn_b[proj * EMBED : proj * EMBED + P].partition_broadcast(P),
+            )
             with nc.allow_non_contiguous_dma(reason="one bias value per partition"):
-                for proj in range(PROJ):
-                    nc.sync.dma_start(
-                        out=bias_cols[:, proj, 1:GROUPS],
-                        in_=c_attn_b[proj * EMBED + P : (proj + 1) * EMBED].rearrange("(g f) -> f g", f=P),
-                    )
-
-        def load_taps(proj):
-            for g in reversed(range(1, GROUPS)):
-                taps = 2 * g + 1
-                for head in range(HEADS_IN_GROUP):
-                    rows = slice(head * HEAD_DIM, (head + 1) * HEAD_DIM)
-                    nc.sync.dma_start(out=tap_w_bf[rows, proj, g, 0:taps], in_=conv_w[proj][g - 1])
-                    nc.sync.dma_start(
-                        out=tap_b[rows, proj, g, 0:1],
-                        in_=conv_b[proj][g - 1].rearrange("(d o) -> d o", o=1),
-                    )
-                nc.vector.tensor_copy(out=tap_w[:, proj, g, 0:taps], in_=tap_w_bf[:, proj, g, 0:taps])
-                nc.vector.tensor_scalar_mul(
-                    out=furthest_diag[:, proj, g, :], in0=ident[:], scalar1=tap_w[:, proj, g, 0:1]
+                nc.sync.dma_start(
+                    out=bias_cols[:, proj, 1:GROUPS],
+                    in_=c_attn_b[proj * EMBED + P : (proj + 1) * EMBED].rearrange("(g f) -> f g", f=P),
                 )
 
-        load_weights(0)
-        first_batch = load_batch(0)
-        load_biases()
-        load_taps(0)
-        for proj in range(1, PROJ):
-            load_weights(proj)
-        for proj in range(1, PROJ):
-            load_taps(proj)
-        quantise_weights(0)
-        quantise_batch(0, first_batch)
-        for proj in range(1, PROJ):
-            quantise_weights(proj)
+        def load_taps(proj, g):
+            taps = 2 * g + 1
+            for head in range(HEADS_IN_GROUP):
+                rows = slice(head * HEAD_DIM, (head + 1) * HEAD_DIM)
+                nc.sync.dma_start(out=tap_w_bf[rows, proj, g, 0:taps], in_=conv_w[proj][g - 1])
+                nc.sync.dma_start(
+                    out=tap_b[rows, proj, g, 0:1],
+                    in_=conv_b[proj][g - 1].rearrange("(d o) -> d o", o=1),
+                )
+            nc.gpsimd.tensor_copy(out=tap_w[:, proj, g, 0:taps], in_=tap_w_bf[:, proj, g, 0:taps])
+            nc.gpsimd.tensor_scalar_mul(out=last_diag[:, proj, g, :], in0=ident[:], scalar1=tap_w[:, proj, g, 0:1])
 
-        x_tiles = [keep.tile([P, X_COLS], F32, name="x_tile%d" % n) for n in range(X_BUFFERS)]
+        x_tiles = [keep.tile([P, X_COLS], F32, name="x_tile%d" % n) for n in range(X_TILES)]
         for x_tile in x_tiles:
             nc.vector.memset(x_tile[:].rearrange("f (t c) -> f t c", c=PADDED)[:, :, 0:1], 0.0)
 
-        def store(b, proj, g, result):
+        load_biases(0)
+        load_taps(0, GROUP_ORDER[0][0])
+        load_weights(0)
+        batch_quarters = {0: load_batch(0)}
+        for proj in range(1, PROJ):
+            load_weights(proj)
+            load_biases(proj)
+        for g in GROUP_ORDER[0][1:]:
+            load_taps(0, g)
+        for proj in range(1, PROJ):
+            for g in GROUP_ORDER[0]:
+                load_taps(proj, g)
+        batch_quarters[1] = load_batch(1)
+
+        jobs = [(b, proj, g) for b in range(BATCH) for proj in range(PROJ) for g in GROUP_ORDER[b]]
+        products = {}
+        job_terms = {}
+
+        def x_of(job):
+            return x_tiles[jobs.index(job) % X_TILES]
+
+        def weight(job, back):
+            b, proj, g = job
+            taps = 2 * g + 1
+            return tap_w[:, proj, g, taps - 1 - back : taps - back]
+
+        def store(b, proj, g, bank, result):
             heads = slice(g * HEADS_IN_GROUP, (g + 1) * HEADS_IN_GROUP)
-            nc.sync.dma_start(
-                out=outs[proj][b, heads, :, :].rearrange("h (p t) d -> p h (t d)", t=BLOCKS),
-                in_=result[:].rearrange("p h t d -> p h (t d)"),
-            )
+            first = bank * BANK_BLOCKS
+            out_view = outs[proj][b, heads, :, :].rearrange("h (p t) d -> p h t d", t=BLOCKS)
+            nc.sync.dma_start(out=out_view[:, :, first : first + BANK_BLOCKS, :], in_=result[:])
 
         def plain_group(b, proj):
-            result = results.tile([P, HEADS_IN_GROUP, BLOCKS, HEAD_DIM], F32)
             w_cols = slice(proj * EMBED, proj * EMBED + P)
             for bank in range(BANKS):
-                first = bank * BANK_BLOCKS
-                by_token = tok_psum.tile([P, BANK_BLOCKS, P], F32, tag="tok")
+                by_token = project_psum.tile([P, BANK_BLOCKS, P], F32, tag="project")
                 for i in range(BANK_BLOCKS):
-                    x_cols = slice(b * SEQ + (first + i) * P, b * SEQ + (first + i + 1) * P)
+                    first_col = b * SEQ + (bank * BANK_BLOCKS + i) * P
                     nc.tensor.matmul_mx(
                         out=by_token[:, i, :],
-                        lhsT=x_codes[:, x_cols].bitcast(FP8X4),
-                        lhsT_scale=x_scales[:, x_cols],
+                        lhsT=x_codes[:, first_col : first_col + P].bitcast(FP8X4),
+                        lhsT_scale=x_scales[:, first_col : first_col + P],
                         rhs=w_codes[:, w_cols].bitcast(FP8X4),
                         rhs_scale=w_scales[:, w_cols],
                         start=True,
                         stop=True,
                     )
+                result = results.tile([P, HEADS_IN_GROUP, BANK_BLOCKS, HEAD_DIM], F32, tag="result")
                 nc.vector.tensor_tensor(
-                    out=result[:, :, first : first + BANK_BLOCKS, :],
+                    out=result[:],
                     in0=by_token[:].rearrange("p t (h d) -> p h t d", h=HEADS_IN_GROUP),
                     in1=bias_rows[:, proj, :]
                     .rearrange("p (h d) -> p h d", h=HEADS_IN_GROUP)
@@ -205,124 +220,129 @@ def tile_tranceptionblockattention_pa_t_kernel(
                     .to_broadcast([P, HEADS_IN_GROUP, BANK_BLOCKS, HEAD_DIM]),
                     op=ALU.add,
                 )
-            store(b, proj, 0, result)
+                store(b, proj, 0, bank, result)
 
-        def conv_group(b, proj, g, x_tile):
-            taps = 2 * g + 1
+        def multiply(job, bank):
+            b, proj, g = job
             w_cols = slice(proj * EMBED + g * P, proj * EMBED + (g + 1) * P)
+            x_cols = slice(b * SEQ + bank * BANK_BLOCKS * P, b * SEQ + (bank + 1) * BANK_BLOCKS * P)
+            by_feature = project_psum.tile([P, BANK_BLOCKS, P], F32, tag="project")
+            nc.tensor.matmul_mx(
+                out=by_feature[:].rearrange("f t p -> f (t p)"),
+                lhsT=w_codes[:, w_cols].bitcast(FP8X4),
+                lhsT_scale=w_scales[:, w_cols],
+                rhs=x_codes[:, x_cols].bitcast(FP8X4),
+                rhs_scale=x_scales[:, x_cols],
+                start=True,
+                stop=True,
+            )
+            products[job, bank] = by_feature
 
-            def weight(back):
-                return tap_w[:, proj, g, taps - 1 - back : taps - back]
+        def write_x(job, bank):
+            b, proj, g = job
+            first = bank * BANK_BLOCKS
+            x_blocks = x_of(job)[:].rearrange("f (t c) -> f t c", c=PADDED)
+            nc.scalar.activation(
+                out=x_blocks[:, first : first + BANK_BLOCKS, 1:PADDED],
+                in_=products[job, bank][:],
+                func=ACT.Identity,
+                bias=bias_cols[:, proj, g : g + 1],
+                scale=1.0,
+            )
 
+        def start_first_term(job, bank):
+            b, proj, g = job
+            if bank == 0:
+                first_term = first_terms.tile([P, X_COLS], F32)
+                job_terms[job] = [(first_term, 0)]
+            cols = slice(bank * BANK_COLS, (bank + 1) * BANK_COLS)
+            nc.scalar.activation(
+                out=job_terms[job][0][0][:, cols], in_=x_of(job)[:, cols], func=ACT.Identity,
+                scale=weight(job, 0), bias=tap_b[:, proj, g, 0:1],
+            )
+
+        def grow(job):
+            b, proj, g = job
+            taps = 2 * g + 1
+            x_tile = x_of(job)
             x_blocks = x_tile[:].rearrange("f (t c) -> f t c", c=PADDED)
-            for bank in range(BANKS):
-                first = bank * BANK_BLOCKS
-                x_cols = slice(b * SEQ + first * P, b * SEQ + (first + BANK_BLOCKS) * P)
-                by_feature = feat_psum.tile([P, BANK_BLOCKS, P], F32)
-                nc.tensor.matmul_mx(
-                    out=by_feature[:].rearrange("f t p -> f (t p)"),
-                    lhsT=w_codes[:, w_cols].bitcast(FP8X4),
-                    lhsT_scale=w_scales[:, w_cols],
-                    rhs=x_codes[:, x_cols].bitcast(FP8X4),
-                    rhs_scale=x_scales[:, x_cols],
-                    start=True,
-                    stop=True,
-                )
-                nc.scalar.activation(
-                    out=x_blocks[:, first : first + BANK_BLOCKS, 1:PADDED],
-                    in_=by_feature[:],
-                    func=ACT.Identity,
-                    bias=bias_cols[:, proj, g : g + 1],
-                    scale=1.0,
-                )
-
-            n_terms = min(g, MAX_TERMS)
-            term_taps = -(-taps // n_terms)
-            shifted_terms = []
-            for first_back in range(0, taps, term_taps):
-                term = terms.tile([P, X_COLS], F32)
-                if first_back > 0 and g == 2:
-                    nc.vector.tensor_scalar_mul(out=term[:], in0=x_tile[:], scalar1=weight(first_back))
+            for nearer in range(TERM_TAPS, taps, TERM_TAPS):
+                term = other_terms.tile([P, X_COLS], F32)
+                if nearer < taps - 1:
+                    nc.vector.tensor_scalar_mul(out=term[:], in0=x_tile[:], scalar1=weight(job, nearer))
                 else:
-                    nc.scalar.activation(
-                        out=term[:], in_=x_tile[:], func=ACT.Identity, scale=weight(first_back),
-                        bias=(tap_b[:, proj, g, 0:1] if first_back == 0 else 0.0),
+                    kept = (TENSOR_EVERY - 1) * PADDED + 1
+                    nc.vector.tensor_scalar_mul(
+                        out=term[:].rearrange("f (i c) -> f i c", c=TENSOR_EVERY * PADDED)[:, :, 0:kept],
+                        in0=x_tile[:].rearrange("f (i c) -> f i c", c=TENSOR_EVERY * PADDED)[:, :, 0:kept],
+                        scalar1=weight(job, nearer),
                     )
-                shifted_terms.append((term, first_back))
-            for further in range(1, term_taps):
-                growing = [(term, first_back) for term, first_back in shifted_terms if first_back + further < taps]
-                for term, first_back in growing:
-                    back = first_back + further
-                    if back == taps - 1:
-                        nc.vector.scalar_tensor_tensor(
-                            out=term[:, (TENSOR_TAP_BLOCKS - first_back) * PADDED : (BLOCKS - first_back) * PADDED],
-                            in0=x_tile[:, (TENSOR_TAP_BLOCKS - back) * PADDED : (BLOCKS - back) * PADDED],
-                            scalar=weight(back),
-                            in1=term[:, (TENSOR_TAP_BLOCKS - first_back) * PADDED : (BLOCKS - first_back) * PADDED],
-                            op0=ALU.mult, op1=ALU.add,
-                        )
-                    else:
-                        nc.vector.scalar_tensor_tensor(
-                            out=term[:, further * PADDED : X_COLS], in0=x_tile[:, 0 : X_COLS - further * PADDED],
-                            scalar=weight(back), in1=term[:, further * PADDED : X_COLS],
-                            op0=ALU.mult, op1=ALU.add,
-                        )
-                for term, first_back in growing:
-                    back = first_back + further
-                    if back < taps - 1:
-                        term_blocks = term[:].rearrange("f (t c) -> f t c", c=PADDED)
-                        nc.vector.scalar_tensor_tensor(
-                            out=term_blocks[:, 0:further, 1:PADDED], in0=x_blocks[:, BLOCKS - further : BLOCKS, 0:P],
-                            scalar=weight(back), in1=term_blocks[:, 0:further, 1:PADDED],
-                            op0=ALU.mult, op1=ALU.add,
-                        )
-
-            def block_from(back, t):
-                block = t - back
-                if block >= 0:
-                    return slice(block * PADDED + 1, block * PADDED + 1 + P)
-                return slice((block + BLOCKS) * PADDED, (block + BLOCKS) * PADDED + P)
-
-            result = results.tile([P, HEADS_IN_GROUP, BLOCKS, HEAD_DIM], F32)
-            for bank in range(BANKS):
-                first = bank * BANK_BLOCKS
-                by_token = tok_psum.tile([P, BANK_BLOCKS, P], F32, tag="tok")
-                for i in range(BANK_BLOCKS):
-                    t = first + i
-                    if t < TENSOR_TAP_BLOCKS:
-                        nc.tensor.matmul(
-                            out=by_token[:, i, :],
-                            lhsT=x_tile[:, block_from(taps - 1, t)],
-                            rhs=furthest_diag[:, proj, g, :],
-                            start=True,
-                            stop=False,
-                        )
-                    for n, (term, first_back) in enumerate(shifted_terms):
-                        nc.tensor.matmul(
-                            out=by_token[:, i, :],
-                            lhsT=term[:, block_from(first_back, t)],
-                            rhs=ident[:],
-                            is_transpose=True,
-                            start=(n == 0 and t >= TENSOR_TAP_BLOCKS),
-                            stop=(n == len(shifted_terms) - 1),
-                        )
-                nc.scalar.copy(
-                    out=result[:, :, first : first + BANK_BLOCKS, :],
-                    in_=by_token[:].rearrange("p t (h d) -> p h t d", h=HEADS_IN_GROUP),
+                job_terms[job].append((term, nearer))
+            pairs = [(term, nearer) for term, nearer in job_terms[job] if nearer < taps - 1]
+            for term, nearer in pairs:
+                nc.vector.scalar_tensor_tensor(
+                    out=term[:, PADDED:X_COLS], in0=x_tile[:, 0 : X_COLS - PADDED],
+                    scalar=weight(job, nearer + 1), in1=term[:, PADDED:X_COLS],
+                    op0=ALU.mult, op1=ALU.add,
                 )
-            store(b, proj, g, result)
+            for term, nearer in pairs:
+                term_blocks = term[:].rearrange("f (t c) -> f t c", c=PADDED)
+                nc.vector.scalar_tensor_tensor(
+                    out=term_blocks[:, 0:1, 1:PADDED], in0=x_blocks[:, BLOCKS - 1 : BLOCKS, 0:P],
+                    scalar=weight(job, nearer + 1), in1=term_blocks[:, 0:1, 1:PADDED],
+                    op0=ALU.mult, op1=ALU.add,
+                )
 
-        conv_groups_done = 0
-        for b in range(BATCH):
-            if b == 0:
-                for proj in range(PROJ):
-                    plain_group(b, proj)
-            for proj in range(PROJ):
-                for g in reversed(range(1, GROUPS)):
-                    conv_group(b, proj, g, x_tiles[conv_groups_done % X_BUFFERS])
-                    conv_groups_done += 1
-                if proj == 0 and b + 1 < BATCH:
-                    quantise_batch(b + 1, load_batch(b + 1))
-            if b == BATCH - 1:
-                for proj in range(PROJ):
-                    plain_group(b, proj)
+        def finish(job, bank):
+            b, proj, g = job
+            taps = 2 * g + 1
+            by_token = turn_psum.tile([P, BANK_BLOCKS, P], F32, tag="turn")
+            for i in range(BANK_BLOCKS):
+                for n, (term, nearer) in enumerate(job_terms[job]):
+                    block = bank * BANK_BLOCKS + i - nearer
+                    if block >= 0:
+                        first_col = block * PADDED + 1
+                    else:
+                        first_col = (block + BLOCKS) * PADDED
+                    on_tensor = nearer == taps - 1 and block % TENSOR_EVERY == TENSOR_EVERY - 1
+                    nc.tensor.matmul(
+                        out=by_token[:, i, :],
+                        lhsT=(x_of(job) if on_tensor else term)[:, first_col : first_col + P],
+                        rhs=(last_diag[:, proj, g, :] if on_tensor else ident[:]),
+                        is_transpose=(None if on_tensor else True),
+                        start=(n == 0),
+                        stop=(n == len(job_terms[job]) - 1),
+                    )
+            result = results.tile([P, HEADS_IN_GROUP, BANK_BLOCKS, HEAD_DIM], F32, tag="result")
+            nc.scalar.copy(out=result[:], in_=by_token[:].rearrange("p t (h d) -> p h t d", h=HEADS_IN_GROUP))
+            store(b, proj, g, bank, result)
+
+        quantise_weights(0)
+        for bank in range(BANKS):
+            quantise_quarter(0, bank, turn_quarter(batch_quarters[0][bank]))
+        for proj in range(1, PROJ):
+            quantise_weights(proj)
+
+        turned_quarters = []
+        for n in range(-X_AHEAD, len(jobs) + 1):
+            if 0 <= n < len(jobs):
+                grow(jobs[n])
+            for bank in range(BANKS):
+                if n + X_AHEAD < len(jobs):
+                    if bank % MX_RUN == 0:
+                        for next_bank in range(bank, bank + MX_RUN):
+                            multiply(jobs[n + X_AHEAD], next_bank)
+                    write_x(jobs[n + X_AHEAD], bank)
+                if 0 <= n + FIRST_TERM_AHEAD < len(jobs):
+                    start_first_term(jobs[n + FIRST_TERM_AHEAD], bank)
+                if n >= 1:
+                    finish(jobs[n - 1], bank)
+            if n < 0:
+                plain_group(0, n + X_AHEAD)
+            if len(jobs) - X_AHEAD <= n < len(jobs):
+                plain_group(1, n + X_AHEAD - len(jobs))
+            if TURN_FROM_ROUND <= n < TURN_FROM_ROUND + BANKS:
+                turned_quarters.append(turn_quarter(batch_quarters[1][n - TURN_FROM_ROUND]))
+            if n == TURN_FROM_ROUND + BANKS:
+                for bank in range(BANKS):
+                    quantise_quarter(1, bank, turned_quarters[bank])

@@ -29,7 +29,7 @@ X_COLS = BLOCKS * PADDED
 BANK_COLS = BANK_BLOCKS * PADDED
 SLOT = 16
 TERM_TAPS = 2
-TENSOR_EVERY = 4
+TENSOR_EVERY = 2
 MX_RUN = 2
 X_AHEAD = 3
 FIRST_TERM_AHEAD = 2

@@ -28,9 +28,9 @@ PADDED = P + 1
 X_COLS = BLOCKS * PADDED
 BANK_COLS = BANK_BLOCKS * PADDED
 SLOT = 16
-TERM_TAPS = 2
+MAX_FULL_TERMS = 2
 TENSOR_EVERY = 2
-MX_RUN = 2
+MX_RUN = 4
 X_AHEAD = 3
 FIRST_TERM_AHEAD = 2
 X_TILES = X_AHEAD + 2
@@ -264,47 +264,49 @@ def tile_tranceptionblockattention_pa_t_kernel(
         def grow(job):
             b, proj, g = job
             taps = 2 * g + 1
+            term_taps = (taps - 1) // min(g, MAX_FULL_TERMS)
             x_tile = x_of(job)
             x_blocks = x_tile[:].rearrange("f (t c) -> f t c", c=PADDED)
-            for nearer in range(TERM_TAPS, taps, TERM_TAPS):
+            for nearest in range(term_taps, taps, term_taps):
                 term = other_terms.tile([P, X_COLS], F32)
-                if nearer < taps - 1:
-                    nc.vector.tensor_scalar_mul(out=term[:], in0=x_tile[:], scalar1=weight(job, nearer))
+                if nearest < taps - 1:
+                    nc.vector.tensor_scalar_mul(out=term[:], in0=x_tile[:], scalar1=weight(job, nearest))
                 else:
                     kept = (TENSOR_EVERY - 1) * PADDED + 1
                     nc.vector.tensor_scalar_mul(
                         out=term[:].rearrange("f (i c) -> f i c", c=TENSOR_EVERY * PADDED)[:, :, 0:kept],
                         in0=x_tile[:].rearrange("f (i c) -> f i c", c=TENSOR_EVERY * PADDED)[:, :, 0:kept],
-                        scalar1=weight(job, nearer),
+                        scalar1=weight(job, nearest),
                     )
-                job_terms[job].append((term, nearer))
-            pairs = [(term, nearer) for term, nearer in job_terms[job] if nearer < taps - 1]
-            for term, nearer in pairs:
-                nc.vector.scalar_tensor_tensor(
-                    out=term[:, PADDED:X_COLS], in0=x_tile[:, 0 : X_COLS - PADDED],
-                    scalar=weight(job, nearer + 1), in1=term[:, PADDED:X_COLS],
-                    op0=ALU.mult, op1=ALU.add,
-                )
-            for term, nearer in pairs:
-                term_blocks = term[:].rearrange("f (t c) -> f t c", c=PADDED)
-                nc.vector.scalar_tensor_tensor(
-                    out=term_blocks[:, 0:1, 1:PADDED], in0=x_blocks[:, BLOCKS - 1 : BLOCKS, 0:P],
-                    scalar=weight(job, nearer + 1), in1=term_blocks[:, 0:1, 1:PADDED],
-                    op0=ALU.mult, op1=ALU.add,
-                )
+                job_terms[job].append((term, nearest))
+            full_terms = [(term, nearest) for term, nearest in job_terms[job] if nearest < taps - 1]
+            for further in range(1, term_taps):
+                for term, nearest in full_terms:
+                    nc.vector.scalar_tensor_tensor(
+                        out=term[:, further * PADDED : X_COLS], in0=x_tile[:, 0 : X_COLS - further * PADDED],
+                        scalar=weight(job, nearest + further), in1=term[:, further * PADDED : X_COLS],
+                        op0=ALU.mult, op1=ALU.add,
+                    )
+                for term, nearest in full_terms:
+                    term_blocks = term[:].rearrange("f (t c) -> f t c", c=PADDED)
+                    nc.vector.scalar_tensor_tensor(
+                        out=term_blocks[:, 0:further, 1:PADDED], in0=x_blocks[:, BLOCKS - further : BLOCKS, 0:P],
+                        scalar=weight(job, nearest + further), in1=term_blocks[:, 0:further, 1:PADDED],
+                        op0=ALU.mult, op1=ALU.add,
+                    )
 
         def finish(job, bank):
             b, proj, g = job
             taps = 2 * g + 1
             by_token = turn_psum.tile([P, BANK_BLOCKS, P], F32, tag="turn")
             for i in range(BANK_BLOCKS):
-                for n, (term, nearer) in enumerate(job_terms[job]):
-                    block = bank * BANK_BLOCKS + i - nearer
+                for n, (term, nearest) in enumerate(job_terms[job]):
+                    block = bank * BANK_BLOCKS + i - nearest
                     if block >= 0:
                         first_col = block * PADDED + 1
                     else:
                         first_col = (block + BLOCKS) * PADDED
-                    on_tensor = nearer == taps - 1 and block % TENSOR_EVERY == TENSOR_EVERY - 1
+                    on_tensor = nearest == taps - 1 and block % TENSOR_EVERY == TENSOR_EVERY - 1
                     nc.tensor.matmul(
                         out=by_token[:, i, :],
                         lhsT=(x_of(job) if on_tensor else term)[:, first_col : first_col + P],

@@ -21,22 +21,16 @@ HEAD_DIM = 64
 
 P = 128
 PACK = 4
-BLOCKS = SEQ // P
-BANK_BLOCKS = 4
-BANKS = BLOCKS // BANK_BLOCKS
-PADDED = P + 1
-X_COLS = BLOCKS * PADDED
-BANK_COLS = BANK_BLOCKS * PADDED
+PHASES = 4
+PLACES = SEQ // PHASES
+BANKS = SEQ // (PHASES * P)
+PAD = 4
+PADDED_TILES = 8
 SLOT = 16
-MAX_FULL_TERMS = 2
-TENSOR_EVERY = 2
-MX_RUN = 4
-X_AHEAD = 3
-FIRST_TERM_AHEAD = 2
-X_TILES = X_AHEAD + 2
-GROUP_ORDER = [[1, 2, 3], [3, 2, 1]]
-TURN_FROM_ROUND = 1
-assert X_AHEAD == PROJ
+NEG_GROUPS = 2
+NEG_COLS = NEG_GROUPS * P
+
+GROUP_ORDER = [[2, 3, 1], [2, 3, 1]]
 
 FLOPS = 2 * BATCH * SEQ * EMBED * PROJ * EMBED + 2 * BATCH * SEQ * PROJ * P * (3 + 5 + 7)
 
@@ -55,21 +49,37 @@ def tile_tranceptionblockattention_pa_t_kernel(
 
     with ExitStack() as stack:
         keep = stack.enter_context(tc.tile_pool(name="keep", bufs=1))
-        x_in = stack.enter_context(tc.tile_pool(name="x_in", bufs=BANKS))
+        x_in = stack.enter_context(tc.tile_pool(name="x_in", bufs=2 * BANKS))
         stage = stack.enter_context(tc.tile_pool(name="stage", bufs=2))
-        first_terms = stack.enter_context(tc.tile_pool(name="first_terms", bufs=FIRST_TERM_AHEAD + 2))
-        other_terms = stack.enter_context(tc.tile_pool(name="other_terms", bufs=6))
-        results = stack.enter_context(tc.tile_pool(name="results", bufs=2 * BANKS))
-        project_psum = stack.enter_context(tc.psum_pool(name="project_psum", bufs=BANKS))
-        turn_psum = stack.enter_context(tc.psum_pool(name="turn_psum", bufs=BANKS))
+        terms = stack.enter_context(tc.tile_pool(name="terms", bufs=4))
+        results = stack.enter_context(tc.tile_pool(name="results", bufs=12))
+        project_psum = stack.enter_context(tc.psum_pool(name="project_psum", bufs=6))
+        turn_psum = stack.enter_context(tc.psum_pool(name="turn_psum", bufs=2))
         stack.enter_context(tc.manual_schedule())
 
+        bias_rows = keep.tile([P, PROJ, P], BF16)
+        bias_cols = keep.tile([P, PROJ, SLOT], BF16)
+        tap_w_bf = keep.tile([P, PROJ, GROUPS, SLOT], BF16)
+        tap_b = keep.tile([P, PROJ, GROUPS, SLOT], BF16)
+        tap_w = keep.tile([P, PROJ, GROUPS, SLOT], F32)
+        prefix = keep.tile([P, PROJ, GROUPS, SLOT], F32)
+        tap_diff = keep.tile([P, PROJ, GROUPS, SLOT], F32)
+        base = keep.tile([P, PROJ, GROUPS, SLOT], F32)
+        bias_f = keep.tile([P, PROJ, SLOT], F32)
+        corr = keep.tile([P, PROJ, GROUPS, 2, 2, 2], F32)
+        nc.gpsimd.memset(corr[:], 0.0)
+        warm = keep.tile([P, 1], F32)
+        nc.gpsimd.memset(warm[:], 0.0)
+        nc.scalar.activation(out=warm[:], in_=warm[:], func=ACT.Identity, scale=1.0)
+        nc.gpsimd.memset(tap_w_bf[:], 0.0)
         ident = keep.tile([P, P], F32)
         make_identity(nc, ident[:])
 
         w_raw = keep.tile([P, PACK, PROJ * EMBED], BF16)
         w_codes = keep.tile([P, PROJ * EMBED], U32, align_bytes=64)
         w_scales = keep.tile([P, PROJ * EMBED], U8, align_bytes=64)
+        neg_codes = keep.tile([P, PROJ * NEG_COLS], U32, align_bytes=64)
+        neg_scales = keep.tile([P, PROJ * NEG_COLS], U8, align_bytes=64)
 
         def load_weights(proj):
             cols = slice(proj * EMBED, (proj + 1) * EMBED)
@@ -79,73 +89,15 @@ def tile_tranceptionblockattention_pa_t_kernel(
                     in_=c_attn_w[u * 2 * P : (u + 1) * 2 * P, cols].rearrange("(q e) c -> q e c", e=2),
                 )
 
-        def quantise_weights(proj):
-            cols = slice(proj * EMBED, (proj + 1) * EMBED)
-            w_grouped = stage.tile([P, EMBED, PACK], BF16, align_bytes=64)
-            nc.vector.tensor_copy(out=w_grouped[:], in_=w_raw[:, :, cols].rearrange("q j c -> q c j"))
-            nc.vector.quantize_mx(
-                out=w_codes[:, cols].bitcast(FP8X4),
-                scales=w_scales[:, cols],
-                in_=w_grouped[:].rearrange("q c j -> q (c j)"),
-            )
-
-        x_codes = keep.tile([P, BATCH * SEQ], U32, align_bytes=64)
-        x_scales = keep.tile([P, BATCH * SEQ], U8, align_bytes=64)
-        x_view = hidden_states.rearrange("b (p t) k -> b p t k", t=BLOCKS)
+        x_view = hidden_states.rearrange("b (i p r) k -> b i p r k", i=BANKS, r=PHASES)
 
         def load_batch(b):
             quarters = []
             for bank in range(BANKS):
-                first = bank * BANK_BLOCKS
-                x_raw = x_in.tile([P, BANK_BLOCKS, EMBED], BF16)
-                nc.sync.dma_start(out=x_raw[:], in_=x_view[b, :, first : first + BANK_BLOCKS, :])
+                x_raw = x_in.tile([P, PHASES, EMBED], BF16)
+                nc.sync.dma_start(out=x_raw[:], in_=x_view[b, bank])
                 quarters.append(x_raw)
             return quarters
-
-        def turn_quarter(x_raw):
-            x_words = x_raw[:].bitcast(F32)
-            x_grouped = stage.tile([P, BANK_BLOCKS * P, PACK], BF16, align_bytes=64, bufs=BANKS)
-            grouped_words = x_grouped[:].bitcast(F32)
-            for half in range(2):
-                turned = turn_psum.tile([P, 2, 2, P], F32, tag="turn")
-                for i in range(2):
-                    for u in range(2):
-                        nc.tensor.transpose(
-                            turned[:, i, u, :], x_words[:, 2 * half + i, u * P : (u + 1) * P], ident[:]
-                        )
-                nc.scalar.copy(
-                    out=grouped_words[:, half * 2 * P : (half + 1) * 2 * P, :].rearrange(
-                        "q (i p) u -> q i p u", i=2
-                    ),
-                    in_=turned[:].rearrange("q i u p -> q i p u"),
-                )
-            return x_grouped
-
-        def quantise_quarter(b, bank, x_grouped):
-            cols = slice(b * SEQ + bank * BANK_BLOCKS * P, b * SEQ + (bank + 1) * BANK_BLOCKS * P)
-            nc.vector.quantize_mx(
-                out=x_codes[:, cols].bitcast(FP8X4),
-                scales=x_scales[:, cols],
-                in_=x_grouped[:].rearrange("q c j -> q (c j)"),
-            )
-
-        bias_rows = keep.tile([P, PROJ, P], BF16)
-        bias_cols = keep.tile([P, PROJ, SLOT], BF16)
-        tap_w_bf = keep.tile([P, PROJ, GROUPS, SLOT], BF16)
-        tap_b = keep.tile([P, PROJ, GROUPS, SLOT], BF16)
-        tap_w = keep.tile([P, PROJ, GROUPS, SLOT], F32)
-        last_diag = keep.tile([P, PROJ, GROUPS, P], F32)
-
-        def load_biases(proj):
-            nc.sync.dma_start(
-                out=bias_rows[:, proj, :],
-                in_=c_attn_b[proj * EMBED : proj * EMBED + P].partition_broadcast(P),
-            )
-            with nc.allow_non_contiguous_dma(reason="one bias value per partition"):
-                nc.sync.dma_start(
-                    out=bias_cols[:, proj, 1:GROUPS],
-                    in_=c_attn_b[proj * EMBED + P : (proj + 1) * EMBED].rearrange("(g f) -> f g", f=P),
-                )
 
         def load_taps(proj, g):
             taps = 2 * g + 1
@@ -153,198 +105,378 @@ def tile_tranceptionblockattention_pa_t_kernel(
                 rows = slice(head * HEAD_DIM, (head + 1) * HEAD_DIM)
                 nc.sync.dma_start(out=tap_w_bf[rows, proj, g, 0:taps], in_=conv_w[proj][g - 1])
                 nc.sync.dma_start(
-                    out=tap_b[rows, proj, g, 0:1],
-                    in_=conv_b[proj][g - 1].rearrange("(d o) -> d o", o=1),
+                    out=tap_b[rows, proj, g, 0:1], in_=conv_b[proj][g - 1].rearrange("(d o) -> d o", o=1)
                 )
-            nc.gpsimd.tensor_copy(out=tap_w[:, proj, g, 0:taps], in_=tap_w_bf[:, proj, g, 0:taps])
-            nc.gpsimd.tensor_scalar_mul(out=last_diag[:, proj, g, :], in0=ident[:], scalar1=tap_w[:, proj, g, 0:1])
 
-        x_tiles = [keep.tile([P, X_COLS], F32, name="x_tile%d" % n) for n in range(X_TILES)]
-        for x_tile in x_tiles:
-            nc.vector.memset(x_tile[:].rearrange("f (t c) -> f t c", c=PADDED)[:, :, 0:1], 0.0)
+        def load_biases(proj):
+            with nc.allow_non_contiguous_dma(reason="one bias value per partition"):
+                nc.sync.dma_start(
+                    out=bias_cols[:, proj, 1:GROUPS],
+                    in_=c_attn_b[proj * EMBED + P : (proj + 1) * EMBED].rearrange("(g f) -> f g", f=P),
+                )
+            nc.sync.dma_start(
+                out=bias_rows[:, proj, :],
+                in_=c_attn_b[proj * EMBED : proj * EMBED + P].partition_broadcast(P),
+            )
 
-        load_biases(0)
-        load_taps(0, GROUP_ORDER[0][0])
         load_weights(0)
         batch_quarters = {0: load_batch(0)}
-        for proj in range(1, PROJ):
-            load_weights(proj)
-            load_biases(proj)
-        for g in GROUP_ORDER[0][1:]:
+        load_biases(0)
+        for g in range(1, GROUPS):
             load_taps(0, g)
         for proj in range(1, PROJ):
-            for g in GROUP_ORDER[0]:
+            load_weights(proj)
+        for proj in range(1, PROJ):
+            load_biases(proj)
+            for g in range(1, GROUPS):
                 load_taps(proj, g)
         batch_quarters[1] = load_batch(1)
 
-        jobs = [(b, proj, g) for b in range(BATCH) for proj in range(PROJ) for g in GROUP_ORDER[b]]
+        def make_constants(proj):
+            gs = slice(1, GROUPS)
+            nc.gpsimd.tensor_copy(out=tap_w[:, proj, gs, :], in_=tap_w_bf[:, proj, gs, :])
+            nc.gpsimd.tensor_copy(out=bias_f[:, proj, gs], in_=bias_cols[:, proj, gs])
+            for g in range(2, GROUPS):
+                taps = 2 * g + 1
+                nc.gpsimd.tensor_copy(out=tap_diff[:, proj, g, 0:1], in_=tap_w[:, proj, g, 0:1])
+                nc.gpsimd.tensor_tensor(
+                    out=tap_diff[:, proj, g, 1 : g + 1],
+                    in0=tap_w[:, proj, g, 2:taps:2], in1=tap_w[:, proj, g, 1 : taps - 1 : 2], op=ALU.subtract,
+                )
+            nc.gpsimd.tensor_copy(out=prefix[:, proj, gs, 0:1], in_=tap_w[:, proj, gs, 0:1])
+            for n in range(1, 2 * GROUPS - 1):
+                nc.gpsimd.tensor_tensor(
+                    out=prefix[:, proj, gs, n : n + 1], in0=prefix[:, proj, gs, n - 1 : n],
+                    in1=tap_w[:, proj, gs, n : n + 1], op=ALU.add,
+                )
+            last = 2 * GROUPS - 2
+            nc.gpsimd.tensor_tensor(
+                out=base[:, proj, gs, 1:2], in0=prefix[:, proj, gs, last : last + 1],
+                in1=bias_f[:, proj, gs].unsqueeze(2), op=ALU.mult,
+            )
+            nc.gpsimd.tensor_tensor(
+                out=base[:, proj, gs, 0:1], in0=base[:, proj, gs, 1:2], in1=tap_b[:, proj, gs, 0:1], op=ALU.add,
+            )
+            for g in range(1, GROUPS):
+                taps = 2 * g + 1
+                for m in range(g):
+                    n = taps - 2 - 2 * m
+                    nc.gpsimd.tensor_scalar(
+                        out=corr[:, proj, g, 0, m % 2, m // 2 : m // 2 + 1], in0=prefix[:, proj, g, n : n + 1],
+                        scalar1=bias_f[:, proj, g : g + 1], scalar2=-1.0, op0=ALU.mult, op1=ALU.mult,
+                    )
+                    source, sign = (prefix[:, proj, g, 0:1], -1.0) if g == 1 else (tap_w[:, proj, g, n : n + 1], 1.0)
+                    nc.gpsimd.tensor_scalar(
+                        out=corr[:, proj, g, 1, m % 2, m // 2 : m // 2 + 1], in0=source,
+                        scalar1=bias_f[:, proj, g : g + 1], scalar2=sign, op0=ALU.mult, op1=ALU.mult,
+                    )
+
+        for proj in range(PROJ):
+            make_constants(proj)
+
+        padded_tiles = [keep.tile([P, 2, PAD + PLACES], F32, name="padded_tile%d" % n) for n in range(PADDED_TILES)]
+        for padded_tile in padded_tiles:
+            nc.vector.memset(padded_tile[:, :, PAD - 1 : PAD], 0.0)
+
+        w_stage = {}
+
+        def group_weights(proj):
+            cols = slice(proj * EMBED, (proj + 1) * EMBED)
+            w_grouped = stage.tile([P, EMBED, PACK], BF16, align_bytes=64)
+            nc.vector.tensor_copy(out=w_grouped[:], in_=w_raw[:, :, cols].rearrange("q j c -> q c j"))
+            w_stage[proj] = w_grouped
+
+        def negate_weights(proj):
+            negated = stage.tile([P, NEG_COLS, PACK], BF16, align_bytes=64)
+            nc.vector.tensor_scalar_mul(out=negated[:], in0=w_stage[proj][:, EMBED - NEG_COLS : EMBED, :], scalar1=-1.0)
+            w_stage[proj, "neg"] = negated
+
+        def quantise_weights(proj):
+            cols = slice(proj * EMBED, (proj + 1) * EMBED)
+            nc.vector.quantize_mx(
+                out=w_codes[:, cols].bitcast(FP8X4), scales=w_scales[:, cols],
+                in_=w_stage[proj][:].rearrange("q c j -> q (c j)"),
+            )
+
+        def quantise_negated(proj):
+            cols = slice(proj * NEG_COLS, (proj + 1) * NEG_COLS)
+            nc.vector.quantize_mx(
+                out=neg_codes[:, cols].bitcast(FP8X4), scales=neg_scales[:, cols],
+                in_=w_stage[proj, "neg"][:].rearrange("q c j -> q (c j)"),
+            )
+
+        x_codes = keep.tile([P, BATCH * SEQ], U32, align_bytes=64)
+        x_scales = keep.tile([P, BATCH * SEQ], U8, align_bytes=64)
+        x_stage = {}
+
+        def turn_pair(b, n, copy):
+            i, pair = n // 2, n % 2
+            if n % 4 == 0:
+                x_grouped = stage.tile([P, PHASES, 2 * P, PACK], BF16, align_bytes=64)
+                x_stage[b, i // 2] = x_grouped
+            words = x_stage[b, i // 2][:].bitcast(F32)
+            x_words = batch_quarters[b][i][:].bitcast(F32)
+            turned = turn_psum.tile([P, 2, 2, P], F32, tag="turn")
+            for j in range(2):
+                for u in range(2):
+                    nc.tensor.transpose(
+                        turned[:, j, u, :], x_words[:, 2 * pair + j, u * P : (u + 1) * P], ident[:]
+                    )
+            first = (i % 2) * P
+            copy(
+                out=words[:, 2 * pair : 2 * pair + 2, first : first + P, :],
+                in_=turned[:].rearrange("q j u p -> q j p u"),
+            )
+
+        def quantise_tokens(b, half, r):
+            first = b * SEQ + r * PLACES + half * 2 * P
+            cols = slice(first, first + 2 * P)
+            nc.vector.quantize_mx(
+                out=x_codes[:, cols].bitcast(FP8X4), scales=x_scales[:, cols],
+                in_=x_stage[b, half][:, r].rearrange("q c j -> q (c j)"),
+            )
+
+        signals = []
+        for b in range(BATCH):
+            for proj in range(PROJ):
+                plain = [(b, proj, 0, h) for h in range(2)]
+                convs = []
+                for g in GROUP_ORDER[b]:
+                    convs += [(b, proj, g, name) for name in (["even", "odd"] if g == 1 else ["even", "odd", "diff"])]
+                signals += plain + convs if b == 0 else convs + plain
+
         products = {}
         job_terms = {}
+        padded_used = []
 
-        def x_of(job):
-            return x_tiles[jobs.index(job) % X_TILES]
+        def mx(out, lhs_codes, lhs_scales, lhs_cols, rhs_codes, rhs_scales, rhs_cols, start, stop):
+            nc.tensor.matmul_mx(
+                out=out,
+                lhsT=lhs_codes[:, lhs_cols].bitcast(FP8X4), lhsT_scale=lhs_scales[:, lhs_cols],
+                rhs=rhs_codes[:, rhs_cols].bitcast(FP8X4), rhs_scale=rhs_scales[:, rhs_cols],
+                start=start, stop=stop,
+            )
 
-        def weight(job, back):
-            b, proj, g = job
-            taps = 2 * g + 1
-            return tap_w[:, proj, g, taps - 1 - back : taps - back]
+        def multiply(signal):
+            b, proj, g, name = signal
+            banks = []
+            for h in range(2):
+                bank = project_psum.tile([P, PLACES], F32, tag="project")
+                if g == 0:
+                    w_cols = slice(proj * EMBED, proj * EMBED + P)
+                    for r in range(PHASES):
+                        col = b * SEQ + r * PLACES + (2 * name + h) * P
+                        mx(
+                            bank[:, r * P : (r + 1) * P], x_codes, x_scales, slice(col, col + P),
+                            w_codes, w_scales, w_cols, True, True,
+                        )
+                else:
+                    first = proj * EMBED + g * P
+                    w_cols = slice(first, first + P)
+                    even_first = b * SEQ + 2 * h * PLACES
+                    even = slice(even_first, even_first + PLACES)
+                    odd = slice(even_first + PLACES, even_first + 2 * PLACES)
+                    if name == "diff":
+                        first = proj * NEG_COLS + (g - 2) * P
+                        mx(bank[:], neg_codes, neg_scales, slice(first, first + P), x_codes, x_scales, even, True, False)
+                        mx(bank[:], w_codes, w_scales, w_cols, x_codes, x_scales, odd, False, True)
+                    else:
+                        mx(bank[:], w_codes, w_scales, w_cols, x_codes, x_scales, even if name == "even" else odd, True, True)
+                banks.append(bank)
+            products[signal] = banks
+
+        def weight(proj, g, back):
+            n = 2 * g - back
+            return tap_w[:, proj, g, n : n + 1]
+
+        def diff_weight(proj, g, i):
+            return tap_diff[:, proj, g, g - i : g - i + 1]
+
+        def main_term(job, n):
+            return job_terms[job][0][:, n]
+
+        def padded_term(job, n):
+            return job_terms[job][n][:, :, PAD:]
+
+        def plan(signal):
+            b, proj, g, name = signal
+            job = signal[:3]
+            bias = base[:, proj, g, 0:1]
+            if g == 0:
+                return [], []
+            if g == 1:
+                y0, y1 = main_term(job, 0), main_term(job, 1)
+                if name == "even":
+                    return (
+                        [(y0, weight(proj, g, 0), bias), (y1, weight(proj, g, 1), bias)],
+                        [(y0, 1, weight(proj, g, 2))],
+                    )
+                return [], [(y1, 0, weight(proj, g, 0)), (y0, 1, weight(proj, g, 1)), (y1, 1, weight(proj, g, 2))]
+            if name == "even":
+                term = main_term(job, 0)
+                return [(term, weight(proj, g, 0), bias)], [(term, i, weight(proj, g, 2 * i)) for i in range(1, g + 1)]
+            if name == "odd":
+                term = padded_term(job, 1)
+                return [(term, weight(proj, g, 1), None)], [(term, i, weight(proj, g, 2 * i + 1)) for i in range(1, g)]
+            term = main_term(job, 1)
+            if g == 2:
+                return [(term, diff_weight(proj, g, 0), None)], [(term, i, diff_weight(proj, g, i)) for i in (1, 2)]
+            late = padded_term(job, 2)
+            return (
+                [(term, diff_weight(proj, g, 0), None), (late, diff_weight(proj, g, 1), None)],
+                [(term, 2, diff_weight(proj, g, 2)), (late, 2, diff_weight(proj, g, 3))],
+            )
+
+        def open_job(signal):
+            g, name = signal[2:]
+            if g and name == "even":
+                main = terms.tile([P, 2, 2, PLACES], F32, tag="main")
+                mine = [main]
+                for n in range(g - 1):
+                    mine.append(padded_tiles[len(padded_used) % PADDED_TILES])
+                    padded_used.append(signal)
+                job_terms[signal[:3]] = mine
+
+        def starts(signal):
+            open_job(signal)
+
+            def start(term, h, scale, bias):
+                if bias is None:
+                    nc.scalar.activation(out=term[:, h, :], in_=products[signal][h][:], func=ACT.Copy, scale=scale)
+                else:
+                    nc.scalar.activation(
+                        out=term[:, h, :], in_=products[signal][h][:], func=ACT.Identity, scale=scale, bias=bias
+                    )
+
+            return [
+                (lambda term=term, h=h, scale=scale, bias=bias: start(term, h, scale, bias))
+                for h in range(2) for term, scale, bias in plan(signal)[0]
+            ]
+
+        def last_of_job(signal):
+            return signal[3] == ("odd" if signal[2] == 1 else "diff")
+
+        def add_taps(signal):
+            b, proj, g, name = signal
+            for h in range(2):
+                for term, i, scalar in plan(signal)[1]:
+                    on, places = (h + i) % 2, (h + i) // 2
+                    out = term[:, on, places:PLACES]
+                    nc.vector.scalar_tensor_tensor(
+                        out=out, in0=products[signal][h][:, 0 : PLACES - places], scalar=scalar, in1=out,
+                        op0=ALU.mult, op1=ALU.add,
+                    )
+            if last_of_job(signal):
+                early = job_terms[signal[:3]][0][:, :, :, 0:2]
+                nc.vector.tensor_tensor(out=early, in0=early, in1=corr[:, proj, g], op=ALU.add)
 
         def store(b, proj, g, bank, result):
             heads = slice(g * HEADS_IN_GROUP, (g + 1) * HEADS_IN_GROUP)
-            first = bank * BANK_BLOCKS
-            out_view = outs[proj][b, heads, :, :].rearrange("h (p t) d -> p h t d", t=BLOCKS)
-            nc.sync.dma_start(out=out_view[:, :, first : first + BANK_BLOCKS, :], in_=result[:])
+            out_view = outs[proj][b, heads].rearrange("h (i p r) d -> i p h r d", i=BANKS, r=PHASES)
+            nc.sync.dma_start(out=out_view[bank], in_=result[:])
 
-        def plain_group(b, proj):
-            w_cols = slice(proj * EMBED, proj * EMBED + P)
-            for bank in range(BANKS):
-                by_token = project_psum.tile([P, BANK_BLOCKS, P], F32, tag="project")
-                for i in range(BANK_BLOCKS):
-                    first_col = b * SEQ + (bank * BANK_BLOCKS + i) * P
-                    nc.tensor.matmul_mx(
-                        out=by_token[:, i, :],
-                        lhsT=x_codes[:, first_col : first_col + P].bitcast(FP8X4),
-                        lhsT_scale=x_scales[:, first_col : first_col + P],
-                        rhs=w_codes[:, w_cols].bitcast(FP8X4),
-                        rhs_scale=w_scales[:, w_cols],
-                        start=True,
-                        stop=True,
-                    )
-                result = results.tile([P, HEADS_IN_GROUP, BANK_BLOCKS, HEAD_DIM], F32, tag="result")
+        def add_plain(signal):
+            b, proj, g, name = signal
+            for h in range(2):
+                result = results.tile([P, HEADS_IN_GROUP, PHASES, HEAD_DIM], F32, tag="result")
                 nc.vector.tensor_tensor(
                     out=result[:],
-                    in0=by_token[:].rearrange("p t (h d) -> p h t d", h=HEADS_IN_GROUP),
-                    in1=bias_rows[:, proj, :]
-                    .rearrange("p (h d) -> p h d", h=HEADS_IN_GROUP)
-                    .unsqueeze(2)
-                    .to_broadcast([P, HEADS_IN_GROUP, BANK_BLOCKS, HEAD_DIM]),
+                    in0=products[signal][h][:].rearrange("p (r h d) -> p h r d", r=PHASES, h=HEADS_IN_GROUP),
+                    in1=bias_rows[:, proj, :].rearrange("p (h d) -> p h d", h=HEADS_IN_GROUP)
+                    .unsqueeze(2).to_broadcast([P, HEADS_IN_GROUP, PHASES, HEAD_DIM]),
                     op=ALU.add,
                 )
-                store(b, proj, 0, bank, result)
+                store(b, proj, 0, 2 * name + h, result)
 
-        def multiply(job, bank):
-            b, proj, g = job
-            w_cols = slice(proj * EMBED + g * P, proj * EMBED + (g + 1) * P)
-            x_cols = slice(b * SEQ + bank * BANK_BLOCKS * P, b * SEQ + (bank + 1) * BANK_BLOCKS * P)
-            by_feature = project_psum.tile([P, BANK_BLOCKS, P], F32, tag="project")
-            nc.tensor.matmul_mx(
-                out=by_feature[:].rearrange("f t p -> f (t p)"),
-                lhsT=w_codes[:, w_cols].bitcast(FP8X4),
-                lhsT_scale=w_scales[:, w_cols],
-                rhs=x_codes[:, x_cols].bitcast(FP8X4),
-                rhs_scale=x_scales[:, x_cols],
-                start=True,
-                stop=True,
-            )
-            products[job, bank] = by_feature
+        def turn_terms(job, bank):
+            g = job[2]
+            by_token = turn_psum.tile([P, PHASES, P], F32, tag="turn")
+            first = bank * P
 
-        def write_x(job, bank):
-            b, proj, g = job
-            first = bank * BANK_BLOCKS
-            x_blocks = x_of(job)[:].rearrange("f (t c) -> f t c", c=PADDED)
-            nc.scalar.activation(
-                out=x_blocks[:, first : first + BANK_BLOCKS, 1:PADDED],
-                in_=products[job, bank][:],
-                func=ACT.Identity,
-                bias=bias_cols[:, proj, g : g + 1],
-                scale=1.0,
-            )
+            def here(term, h):
+                return term[:, h, first : first + P]
 
-        def start_first_term(job, bank):
-            b, proj, g = job
-            if bank == 0:
-                first_term = first_terms.tile([P, X_COLS], F32)
-                job_terms[job] = [(first_term, 0)]
-            cols = slice(bank * BANK_COLS, (bank + 1) * BANK_COLS)
-            nc.scalar.activation(
-                out=job_terms[job][0][0][:, cols], in_=x_of(job)[:, cols], func=ACT.Identity,
-                scale=weight(job, 0), bias=tap_b[:, proj, g, 0:1],
-            )
+            def one_back(tile, h):
+                if h:
+                    return tile[:, 0, PAD + first : PAD + first + P]
+                return tile[:, 1, PAD - 1 + first : PAD - 1 + first + P]
 
-        def grow(job):
-            b, proj, g = job
-            taps = 2 * g + 1
-            term_taps = (taps - 1) // min(g, MAX_FULL_TERMS)
-            x_tile = x_of(job)
-            x_blocks = x_tile[:].rearrange("f (t c) -> f t c", c=PADDED)
-            for nearest in range(term_taps, taps, term_taps):
-                term = other_terms.tile([P, X_COLS], F32)
-                if nearest < taps - 1:
-                    nc.vector.tensor_scalar_mul(out=term[:], in0=x_tile[:], scalar1=weight(job, nearest))
+            for r in range(PHASES):
+                h, parity = divmod(r, 2)
+                mine = job_terms[job]
+                if g == 1:
+                    parts = [here(main_term(job, parity), h)]
+                elif parity == 0:
+                    parts = [here(main_term(job, 0), h), one_back(mine[1], h)]
                 else:
-                    kept = (TENSOR_EVERY - 1) * PADDED + 1
-                    nc.vector.tensor_scalar_mul(
-                        out=term[:].rearrange("f (i c) -> f i c", c=TENSOR_EVERY * PADDED)[:, :, 0:kept],
-                        in0=x_tile[:].rearrange("f (i c) -> f i c", c=TENSOR_EVERY * PADDED)[:, :, 0:kept],
-                        scalar1=weight(job, nearest),
-                    )
-                job_terms[job].append((term, nearest))
-            full_terms = [(term, nearest) for term, nearest in job_terms[job] if nearest < taps - 1]
-            for further in range(1, term_taps):
-                for term, nearest in full_terms:
-                    nc.vector.scalar_tensor_tensor(
-                        out=term[:, further * PADDED : X_COLS], in0=x_tile[:, 0 : X_COLS - further * PADDED],
-                        scalar=weight(job, nearest + further), in1=term[:, further * PADDED : X_COLS],
-                        op0=ALU.mult, op1=ALU.add,
-                    )
-                for term, nearest in full_terms:
-                    term_blocks = term[:].rearrange("f (t c) -> f t c", c=PADDED)
-                    nc.vector.scalar_tensor_tensor(
-                        out=term_blocks[:, 0:further, 1:PADDED], in0=x_blocks[:, BLOCKS - further : BLOCKS, 0:P],
-                        scalar=weight(job, nearest + further), in1=term_blocks[:, 0:further, 1:PADDED],
-                        op0=ALU.mult, op1=ALU.add,
-                    )
-
-        def finish(job, bank):
-            b, proj, g = job
-            taps = 2 * g + 1
-            by_token = turn_psum.tile([P, BANK_BLOCKS, P], F32, tag="turn")
-            for i in range(BANK_BLOCKS):
-                for n, (term, nearest) in enumerate(job_terms[job]):
-                    block = bank * BANK_BLOCKS + i - nearest
-                    if block >= 0:
-                        first_col = block * PADDED + 1
-                    else:
-                        first_col = (block + BLOCKS) * PADDED
-                    on_tensor = nearest == taps - 1 and block % TENSOR_EVERY == TENSOR_EVERY - 1
+                    parts = [here(main_term(job, 0), h), here(padded_term(job, 1), h), here(main_term(job, 1), h)]
+                    parts += [one_back(late, h) for late in mine[2:]]
+                for n, part in enumerate(parts):
                     nc.tensor.matmul(
-                        out=by_token[:, i, :],
-                        lhsT=(x_of(job) if on_tensor else term)[:, first_col : first_col + P],
-                        rhs=(last_diag[:, proj, g, :] if on_tensor else ident[:]),
-                        is_transpose=(None if on_tensor else True),
-                        start=(n == 0),
-                        stop=(n == len(job_terms[job]) - 1),
+                        out=by_token[:, r, :], lhsT=part, rhs=ident[:], is_transpose=True,
+                        start=(n == 0), stop=(n == len(parts) - 1),
                     )
-            result = results.tile([P, HEADS_IN_GROUP, BANK_BLOCKS, HEAD_DIM], F32, tag="result")
-            nc.scalar.copy(out=result[:], in_=by_token[:].rearrange("p t (h d) -> p h t d", h=HEADS_IN_GROUP))
+            return by_token
+
+        def copy_out(job, bank, by_token):
+            b, proj, g = job
+            result = results.tile([P, HEADS_IN_GROUP, PHASES, HEAD_DIM], F32, tag="result")
+            nc.scalar.copy(out=result[:], in_=by_token[:].rearrange("p r (h d) -> p h r d", h=HEADS_IN_GROUP))
             store(b, proj, g, bank, result)
 
+        group_weights(0)
+        negate_weights(0)
         quantise_weights(0)
-        for bank in range(BANKS):
-            quantise_quarter(0, bank, turn_quarter(batch_quarters[0][bank]))
-        for proj in range(1, PROJ):
-            quantise_weights(proj)
+        quantise_negated(0)
+        for n in range(2 * BANKS):
+            turn_pair(0, n, nc.scalar.copy if n % 2 else nc.vector.tensor_copy)
+            if n % 4 == 3:
+                for r in range(PHASES):
+                    quantise_tokens(0, n // 4, r)
 
-        turned_quarters = []
-        for n in range(-X_AHEAD, len(jobs) + 1):
-            if 0 <= n < len(jobs):
-                grow(jobs[n])
-            for bank in range(BANKS):
-                if n + X_AHEAD < len(jobs):
-                    if bank % MX_RUN == 0:
-                        for next_bank in range(bank, bank + MX_RUN):
-                            multiply(jobs[n + X_AHEAD], next_bank)
-                    write_x(jobs[n + X_AHEAD], bank)
-                if 0 <= n + FIRST_TERM_AHEAD < len(jobs):
-                    start_first_term(jobs[n + FIRST_TERM_AHEAD], bank)
-                if n >= 1:
-                    finish(jobs[n - 1], bank)
-            if n < 0:
-                plain_group(0, n + X_AHEAD)
-            if len(jobs) - X_AHEAD <= n < len(jobs):
-                plain_group(1, n + X_AHEAD - len(jobs))
-            if TURN_FROM_ROUND <= n < TURN_FROM_ROUND + BANKS:
-                turned_quarters.append(turn_quarter(batch_quarters[1][n - TURN_FROM_ROUND]))
-            if n == TURN_FROM_ROUND + BANKS:
-                for bank in range(BANKS):
-                    quantise_quarter(1, bank, turned_quarters[bank])
+        extras = []
+        for proj in range(1, PROJ):
+            for work in (group_weights, negate_weights, quantise_weights, quantise_negated):
+                extras.append(lambda work=work, proj=proj: work(proj))
+
+        def quantise_half(half):
+            for r in range(PHASES):
+                quantise_tokens(1, half, r)
+
+        for n in range(2 * BANKS):
+            extras.append(lambda n=n: turn_pair(1, n, nc.scalar.copy))
+            if n % 4 == 3:
+                extras.append(lambda n=n: quantise_half(n // 4))
+
+        turn_queue = []
+        credit = 0
+        for k in range(-2, len(signals)):
+            begin = starts(signals[k + 1]) if 0 <= k + 1 < len(signals) else []
+            ends = []
+            if k >= 0:
+                work = max(len(plan(signals[k])[1]), 1) * 2
+                credit = min(credit + work * 1.25 - len(begin), 2)
+                while turn_queue and turn_queue[0][0] < k - 1 and credit >= 1:
+                    ends.append(turn_queue.pop(0)[1:])
+                    credit -= 1
+            turned = [turn_terms(*end) for end in ends[:2]]
+            if k + 2 < len(signals):
+                multiply(signals[k + 2])
+            for n in range(max(len(begin), len(ends))):
+                if n < len(begin):
+                    begin[n]()
+                if n < len(ends):
+                    if n >= 2:
+                        turned.append(turn_terms(*ends[n]))
+                    copy_out(*ends[n], turned[n])
+            if k >= 0:
+                if signals[k][2] == 0:
+                    add_plain(signals[k])
+                else:
+                    add_taps(signals[k])
+                if last_of_job(signals[k]):
+                    turn_queue += [(k, signals[k][:3], bank) for bank in range(BANKS)]
+                if extras and k >= 1:
+                    extras.pop(0)()
+        for k, job, bank in turn_queue:
+            copy_out(job, bank, turn_terms(job, bank))

@@ -26,11 +26,17 @@ PLACES = SEQ // PHASES
 BANKS = SEQ // (PHASES * P)
 PAD = 4
 PADDED_TILES = 8
+SECOND_DIFF = (3,)
+CREDIT = 1.3
+CAP = 2
+LAG = 1
+LONE = True
+CLOSING = 2
 SLOT = 16
 NEG_GROUPS = 2
 NEG_COLS = NEG_GROUPS * P
 
-GROUP_ORDER = [[2, 3, 1], [2, 3, 1]]
+GROUP_ORDER = [[1, 2, 3], [1, 2, 3]]
 
 FLOPS = 2 * BATCH * SEQ * EMBED * PROJ * EMBED + 2 * BATCH * SEQ * PROJ * P * (3 + 5 + 7)
 
@@ -91,51 +97,54 @@ def tile_tranceptionblockattention_pa_t_kernel(
 
         x_view = hidden_states.rearrange("b (i p r) k -> b i p r k", i=BANKS, r=PHASES)
 
-        def load_batch(b):
-            quarters = []
-            for bank in range(BANKS):
-                x_raw = x_in.tile([P, PHASES, EMBED], BF16)
-                nc.sync.dma_start(out=x_raw[:], in_=x_view[b, bank])
-                quarters.append(x_raw)
-            return quarters
+        def load_quarter(b, i):
+            x_raw = x_in.tile([P, PHASES, EMBED], BF16)
+            nc.sync.dma_start(out=x_raw[:], in_=x_view[b, i])
+            return x_raw
 
-        def load_taps(proj, g):
+        def load_taps(proj, g, queue=nc.sync):
             taps = 2 * g + 1
             for head in range(HEADS_IN_GROUP):
                 rows = slice(head * HEAD_DIM, (head + 1) * HEAD_DIM)
-                nc.sync.dma_start(out=tap_w_bf[rows, proj, g, 0:taps], in_=conv_w[proj][g - 1])
-                nc.sync.dma_start(
+                queue.dma_start(out=tap_w_bf[rows, proj, g, 0:taps], in_=conv_w[proj][g - 1])
+                queue.dma_start(
                     out=tap_b[rows, proj, g, 0:1], in_=conv_b[proj][g - 1].rearrange("(d o) -> d o", o=1)
                 )
 
-        def load_biases(proj):
+        def load_biases(proj, queue=nc.sync):
             with nc.allow_non_contiguous_dma(reason="one bias value per partition"):
-                nc.sync.dma_start(
-                    out=bias_cols[:, proj, 1:GROUPS],
+                queue.dma_start(
+                    out=bias_cols[:, proj, 0 : GROUPS - 1],
                     in_=c_attn_b[proj * EMBED + P : (proj + 1) * EMBED].rearrange("(g f) -> f g", f=P),
                 )
+
+        def load_bias_rows(proj):
             nc.sync.dma_start(
                 out=bias_rows[:, proj, :],
                 in_=c_attn_b[proj * EMBED : proj * EMBED + P].partition_broadcast(P),
             )
 
+        load_biases(0, nc.scalar)
+        load_taps(0, GROUP_ORDER[0][0], nc.scalar)
+        batch_quarters = {0: [load_quarter(0, 0)]}
         load_weights(0)
-        batch_quarters = {0: load_batch(0)}
-        load_biases(0)
-        for g in range(1, GROUPS):
+        batch_quarters[0] += [load_quarter(0, i) for i in range(1, BANKS)]
+        for g in GROUP_ORDER[0][1:]:
             load_taps(0, g)
+        load_bias_rows(0)
         for proj in range(1, PROJ):
             load_weights(proj)
         for proj in range(1, PROJ):
             load_biases(proj)
+            load_bias_rows(proj)
             for g in range(1, GROUPS):
                 load_taps(proj, g)
-        batch_quarters[1] = load_batch(1)
+        batch_quarters[1] = [load_quarter(1, i) for i in range(BANKS)]
 
         def make_constants(proj):
             gs = slice(1, GROUPS)
             nc.gpsimd.tensor_copy(out=tap_w[:, proj, gs, :], in_=tap_w_bf[:, proj, gs, :])
-            nc.gpsimd.tensor_copy(out=bias_f[:, proj, gs], in_=bias_cols[:, proj, gs])
+            nc.gpsimd.tensor_copy(out=bias_f[:, proj, gs], in_=bias_cols[:, proj, 0 : GROUPS - 1])
             for g in range(2, GROUPS):
                 taps = 2 * g + 1
                 nc.gpsimd.tensor_copy(out=tap_diff[:, proj, g, 0:1], in_=tap_w[:, proj, g, 0:1])
@@ -143,20 +152,30 @@ def tile_tranceptionblockattention_pa_t_kernel(
                     out=tap_diff[:, proj, g, 1 : g + 1],
                     in0=tap_w[:, proj, g, 2:taps:2], in1=tap_w[:, proj, g, 1 : taps - 1 : 2], op=ALU.subtract,
                 )
+            width = GROUPS
+            source = tap_w
+            while width:
+                nc.gpsimd.tensor_tensor(
+                    out=base[:, proj, gs, 0:width], in0=source[:, proj, gs, 0:width],
+                    in1=source[:, proj, gs, width : 2 * width], op=ALU.add,
+                )
+                source = base
+                width //= 2
+            nc.gpsimd.tensor_tensor(
+                out=base[:, proj, gs, 0:1], in0=base[:, proj, gs, 0:1], in1=bias_f[:, proj, gs].unsqueeze(2), op=ALU.mult
+            )
+            nc.gpsimd.tensor_tensor(
+                out=base[:, proj, gs, 0:1], in0=base[:, proj, gs, 0:1], in1=tap_b[:, proj, gs, 0:1], op=ALU.add
+            )
+
+        def make_corrections(proj):
+            gs = slice(1, GROUPS)
             nc.gpsimd.tensor_copy(out=prefix[:, proj, gs, 0:1], in_=tap_w[:, proj, gs, 0:1])
-            for n in range(1, 2 * GROUPS - 1):
+            for n in range(1, 2 * GROUPS - 2):
                 nc.gpsimd.tensor_tensor(
                     out=prefix[:, proj, gs, n : n + 1], in0=prefix[:, proj, gs, n - 1 : n],
                     in1=tap_w[:, proj, gs, n : n + 1], op=ALU.add,
                 )
-            last = 2 * GROUPS - 2
-            nc.gpsimd.tensor_tensor(
-                out=base[:, proj, gs, 1:2], in0=prefix[:, proj, gs, last : last + 1],
-                in1=bias_f[:, proj, gs].unsqueeze(2), op=ALU.mult,
-            )
-            nc.gpsimd.tensor_tensor(
-                out=base[:, proj, gs, 0:1], in0=base[:, proj, gs, 1:2], in1=tap_b[:, proj, gs, 0:1], op=ALU.add,
-            )
             for g in range(1, GROUPS):
                 taps = 2 * g + 1
                 for m in range(g):
@@ -171,8 +190,7 @@ def tile_tranceptionblockattention_pa_t_kernel(
                         scalar1=bias_f[:, proj, g : g + 1], scalar2=sign, op0=ALU.mult, op1=ALU.mult,
                     )
 
-        for proj in range(PROJ):
-            make_constants(proj)
+        make_constants(0)
 
         padded_tiles = [keep.tile([P, 2, PAD + PLACES], F32, name="padded_tile%d" % n) for n in range(PADDED_TILES)]
         for padded_tile in padded_tiles:
@@ -185,6 +203,23 @@ def tile_tranceptionblockattention_pa_t_kernel(
             w_grouped = stage.tile([P, EMBED, PACK], BF16, align_bytes=64)
             nc.vector.tensor_copy(out=w_grouped[:], in_=w_raw[:, :, cols].rearrange("q j c -> q c j"))
             w_stage[proj] = w_grouped
+
+        def group_some(proj, part):
+            if part == 0:
+                w_grouped = stage.tile([P, EMBED, PACK], BF16, align_bytes=64)
+                w_stage[proj] = w_grouped
+            first = part * P
+            nc.scalar.copy(
+                out=w_stage[proj][:, first : first + P, :],
+                in_=w_raw[:, :, proj * EMBED + first : proj * EMBED + first + P].rearrange("q j c -> q c j"),
+            )
+
+        def negate_on_scalar(proj):
+            negated = stage.tile([P, NEG_COLS, PACK], BF16, align_bytes=64)
+            nc.scalar.activation(
+                out=negated[:], in_=w_stage[proj][:, EMBED - NEG_COLS : EMBED, :], func=ACT.Copy, scale=-1.0
+            )
+            w_stage[proj, "neg"] = negated
 
         def negate_weights(proj):
             negated = stage.tile([P, NEG_COLS, PACK], BF16, align_bytes=64)
@@ -211,10 +246,10 @@ def tile_tranceptionblockattention_pa_t_kernel(
 
         def turn_pair(b, n, copy):
             i, pair = n // 2, n % 2
-            if n % 4 == 0:
-                x_grouped = stage.tile([P, PHASES, 2 * P, PACK], BF16, align_bytes=64)
-                x_stage[b, i // 2] = x_grouped
-            words = x_stage[b, i // 2][:].bitcast(F32)
+            if n == 0:
+                x_grouped = stage.tile([P, PHASES, PLACES, PACK], BF16, align_bytes=64, bufs=1)
+                x_stage[b] = x_grouped
+            words = x_stage[b][:].bitcast(F32)
             x_words = batch_quarters[b][i][:].bitcast(F32)
             turned = turn_psum.tile([P, 2, 2, P], F32, tag="turn")
             for j in range(2):
@@ -222,18 +257,21 @@ def tile_tranceptionblockattention_pa_t_kernel(
                     nc.tensor.transpose(
                         turned[:, j, u, :], x_words[:, 2 * pair + j, u * P : (u + 1) * P], ident[:]
                     )
-            first = (i % 2) * P
+            first = i * P
             copy(
                 out=words[:, 2 * pair : 2 * pair + 2, first : first + P, :],
                 in_=turned[:].rearrange("q j u p -> q j p u"),
             )
 
-        def quantise_tokens(b, half, r):
-            first = b * SEQ + r * PLACES + half * 2 * P
-            cols = slice(first, first + 2 * P)
+        def quantise_tokens(b, r, half=None):
+            if half is None:
+                places = slice(0, PLACES)
+            else:
+                places = slice(half * 2 * P, (half + 1) * 2 * P)
+            cols = slice(b * SEQ + r * PLACES + places.start, b * SEQ + r * PLACES + places.stop)
             nc.vector.quantize_mx(
                 out=x_codes[:, cols].bitcast(FP8X4), scales=x_scales[:, cols],
-                in_=x_stage[b, half][:, r].rearrange("q c j -> q (c j)"),
+                in_=x_stage[b][:, r, places, :].rearrange("q c j -> q (c j)"),
             )
 
         signals = []
@@ -311,6 +349,11 @@ def tile_tranceptionblockattention_pa_t_kernel(
                         [(y0, weight(proj, g, 0), bias), (y1, weight(proj, g, 1), bias)],
                         [(y0, 1, weight(proj, g, 2))],
                     )
+                if LONE:
+                    return (
+                        [(job_terms[job][1][:], weight(proj, g, 0), None)],
+                        [(y0, 1, weight(proj, g, 1)), (y1, 1, weight(proj, g, 2))],
+                    )
                 return [], [(y1, 0, weight(proj, g, 0)), (y0, 1, weight(proj, g, 1)), (y1, 1, weight(proj, g, 2))]
             if name == "even":
                 term = main_term(job, 0)
@@ -319,12 +362,12 @@ def tile_tranceptionblockattention_pa_t_kernel(
                 term = padded_term(job, 1)
                 return [(term, weight(proj, g, 1), None)], [(term, i, weight(proj, g, 2 * i + 1)) for i in range(1, g)]
             term = main_term(job, 1)
-            if g == 2:
-                return [(term, diff_weight(proj, g, 0), None)], [(term, i, diff_weight(proj, g, i)) for i in (1, 2)]
+            if g not in SECOND_DIFF:
+                return [(term, diff_weight(proj, g, 0), None)], [(term, i, diff_weight(proj, g, i)) for i in range(1, g + 1)]
             late = padded_term(job, 2)
             return (
                 [(term, diff_weight(proj, g, 0), None), (late, diff_weight(proj, g, 1), None)],
-                [(term, 2, diff_weight(proj, g, 2)), (late, 2, diff_weight(proj, g, 3))],
+                [(late if i % 2 else term, 2 * (i // 2), diff_weight(proj, g, i)) for i in range(2, g + 1)],
             )
 
         def open_job(signal):
@@ -332,7 +375,10 @@ def tile_tranceptionblockattention_pa_t_kernel(
             if g and name == "even":
                 main = terms.tile([P, 2, 2, PLACES], F32, tag="main")
                 mine = [main]
-                for n in range(g - 1):
+                if g == 1 and LONE:
+                    lone = terms.tile([P, 2, PLACES], F32, tag="lone")
+                    mine.append(lone)
+                for n in range(g > 1 and 1 + (g in SECOND_DIFF)):
                     mine.append(padded_tiles[len(padded_used) % PADDED_TILES])
                     padded_used.append(signal)
                 job_terms[signal[:3]] = mine
@@ -359,16 +405,18 @@ def tile_tranceptionblockattention_pa_t_kernel(
         def add_taps(signal):
             b, proj, g, name = signal
             for h in range(2):
-                for term, i, scalar in plan(signal)[1]:
+                taps = plan(signal)[1]
+                for term, i, scalar in taps[::-1] if h else taps:
                     on, places = (h + i) % 2, (h + i) // 2
                     out = term[:, on, places:PLACES]
                     nc.vector.scalar_tensor_tensor(
                         out=out, in0=products[signal][h][:, 0 : PLACES - places], scalar=scalar, in1=out,
                         op0=ALU.mult, op1=ALU.add,
                     )
-            if last_of_job(signal):
-                early = job_terms[signal[:3]][0][:, :, :, 0:2]
-                nc.vector.tensor_tensor(out=early, in0=early, in1=corr[:, proj, g], op=ALU.add)
+
+        def correct(job):
+            early = job_terms[job][0][:, :, :, 0:2]
+            nc.gpsimd.tensor_tensor(out=early, in0=early, in1=corr[:, job[1], job[2]], op=ALU.add)
 
         def store(b, proj, g, bank, result):
             heads = slice(g * HEADS_IN_GROUP, (g + 1) * HEADS_IN_GROUP)
@@ -406,6 +454,8 @@ def tile_tranceptionblockattention_pa_t_kernel(
                 mine = job_terms[job]
                 if g == 1:
                     parts = [here(main_term(job, parity), h)]
+                    if parity and LONE:
+                        parts.append(here(mine[1], h))
                 elif parity == 0:
                     parts = [here(main_term(job, 0), h), one_back(mine[1], h)]
                 else:
@@ -418,10 +468,10 @@ def tile_tranceptionblockattention_pa_t_kernel(
                     )
             return by_token
 
-        def copy_out(job, bank, by_token):
+        def copy_out(job, bank, by_token, copy=nc.scalar.copy):
             b, proj, g = job
             result = results.tile([P, HEADS_IN_GROUP, PHASES, HEAD_DIM], F32, tag="result")
-            nc.scalar.copy(out=result[:], in_=by_token[:].rearrange("p r (h d) -> p h r d", h=HEADS_IN_GROUP))
+            copy(out=result[:], in_=by_token[:].rearrange("p r (h d) -> p h r d", h=HEADS_IN_GROUP))
             store(b, proj, g, bank, result)
 
         group_weights(0)
@@ -432,22 +482,21 @@ def tile_tranceptionblockattention_pa_t_kernel(
             turn_pair(0, n, nc.scalar.copy if n % 2 else nc.vector.tensor_copy)
             if n % 4 == 3:
                 for r in range(PHASES):
-                    quantise_tokens(0, n // 4, r)
+                    quantise_tokens(0, r, n // 4)
 
-        extras = []
+        extras = [lambda: make_corrections(0)]
         for proj in range(1, PROJ):
-            for work in (group_weights, negate_weights, quantise_weights, quantise_negated):
-                extras.append(lambda work=work, proj=proj: work(proj))
-
-        def quantise_half(half):
-            for r in range(PHASES):
-                quantise_tokens(1, half, r)
-
+            for parts in ((0,), (1,), (2, 3)):
+                extras.append(lambda parts=parts, proj=proj: [group_some(proj, part) for part in parts])
+            extras.append(lambda proj=proj: (negate_on_scalar(proj), quantise_weights(proj)))
+            extras.append(lambda proj=proj: quantise_negated(proj))
+            extras.append(lambda proj=proj: (make_constants(proj), make_corrections(proj)))
         for n in range(2 * BANKS):
             extras.append(lambda n=n: turn_pair(1, n, nc.scalar.copy))
-            if n % 4 == 3:
-                extras.append(lambda n=n: quantise_half(n // 4))
+        for r in range(PHASES):
+            extras.append(lambda r=r: quantise_tokens(1, r))
 
+        uncorrected = []
         turn_queue = []
         credit = 0
         for k in range(-2, len(signals)):
@@ -455,8 +504,9 @@ def tile_tranceptionblockattention_pa_t_kernel(
             ends = []
             if k >= 0:
                 work = max(len(plan(signals[k])[1]), 1) * 2
-                credit = min(credit + work * 1.25 - len(begin), 2)
-                while turn_queue and turn_queue[0][0] < k - 1 and credit >= 1:
+                closing = k >= len(signals) - 2
+                credit = CLOSING if closing else min(credit + work * CREDIT - len(begin), CAP)
+                while turn_queue and turn_queue[0][0] < k - (1 if closing else LAG) and credit >= 1:
                     ends.append(turn_queue.pop(0)[1:])
                     credit -= 1
             turned = [turn_terms(*end) for end in ends[:2]]
@@ -474,9 +524,14 @@ def tile_tranceptionblockattention_pa_t_kernel(
                     add_plain(signals[k])
                 else:
                     add_taps(signals[k])
+                if uncorrected:
+                    correct(uncorrected.pop(0))
                 if last_of_job(signals[k]):
+                    uncorrected.append(signals[k][:3])
                     turn_queue += [(k, signals[k][:3], bank) for bank in range(BANKS)]
                 if extras and k >= 1:
                     extras.pop(0)()
+        for job in uncorrected:
+            correct(job)
         for k, job, bank in turn_queue:
-            copy_out(job, bank, turn_terms(job, bank))
+            copy_out(job, bank, turn_terms(job, bank), nc.vector.tensor_copy if bank % 2 else nc.scalar.copy)

from contextlib import ExitStack

import concourse.mybir as mybir
from concourse.masks import make_identity

F32 = mybir.dt.float32
BF16 = mybir.dt.bfloat16
U32 = mybir.dt.uint32
U8 = mybir.dt.uint8
FP8X4 = mybir.dt.float8_e4m3fn_x4
ALU = mybir.AluOpType
ACT = mybir.ActivationFunctionType

BATCH = 2
SEQ = 2048
EMBED = 512
PROJ = 3
GROUPS = 4
HEADS_IN_GROUP = 2
HEAD_DIM = 64

P = 128
PACK = 4
PHASES = 4
PLACES = SEQ // PHASES
BANKS = SEQ // (PHASES * P)
PAD = 4
PADDED_TILES = 8
SECOND_DIFF = (3,)
CREDIT = 1.3
CAP = 2
LAG = 1
LONE = True
CLOSING = 2
SLOT = 16
NEG_GROUPS = 2
NEG_COLS = NEG_GROUPS * P

GROUP_ORDER = [[1, 2, 3], [1, 2, 3]]

FLOPS = 2 * BATCH * SEQ * EMBED * PROJ * EMBED + 2 * BATCH * SEQ * PROJ * P * (3 + 5 + 7)


def tile_tranceptionblockattention_pa_t_kernel(
    tc, hidden_states, c_attn_w, c_attn_b,
    qw3, qb3, qw5, qb5, qw7, qb7,
    kw3, kb3, kw5, kb5, kw7, kb7,
    vw3, vb3, vw5, vb5, vw7, vb7,
    out_0, out_1, out_2,
):
    nc = tc.nc
    conv_w = [[qw3, qw5, qw7], [kw3, kw5, kw7], [vw3, vw5, vw7]]
    conv_b = [[qb3, qb5, qb7], [kb3, kb5, kb7], [vb3, vb5, vb7]]
    outs = [out_0, out_1, out_2]

    with ExitStack() as stack:
        keep = stack.enter_context(tc.tile_pool(name="keep", bufs=1))
        x_in = stack.enter_context(tc.tile_pool(name="x_in", bufs=2 * BANKS))
        stage = stack.enter_context(tc.tile_pool(name="stage", bufs=2))
        terms = stack.enter_context(tc.tile_pool(name="terms", bufs=4))
        results = stack.enter_context(tc.tile_pool(name="results", bufs=12))
        project_psum = stack.enter_context(tc.psum_pool(name="project_psum", bufs=6))
        turn_psum = stack.enter_context(tc.psum_pool(name="turn_psum", bufs=2))
        stack.enter_context(tc.manual_schedule())

        bias_rows = keep.tile([P, PROJ, P], BF16)
        bias_cols = keep.tile([P, PROJ, SLOT], BF16)
        tap_w_bf = keep.tile([P, PROJ, GROUPS, SLOT], BF16)
        tap_b = keep.tile([P, PROJ, GROUPS, SLOT], BF16)
        tap_w = keep.tile([P, PROJ, GROUPS, SLOT], F32)
        prefix = keep.tile([P, PROJ, GROUPS, SLOT], F32)
        tap_diff = keep.tile([P, PROJ, GROUPS, SLOT], F32)
        base = keep.tile([P, PROJ, GROUPS, SLOT], F32)
        bias_f = keep.tile([P, PROJ, SLOT], F32)
        corr = keep.tile([P, PROJ, GROUPS, 2, 2, 2], F32)
        nc.gpsimd.memset(corr[:], 0.0)
        warm = keep.tile([P, 1], F32)
        nc.gpsimd.memset(warm[:], 0.0)
        nc.scalar.activation(out=warm[:], in_=warm[:], func=ACT.Identity, scale=1.0)
        nc.gpsimd.memset(tap_w_bf[:], 0.0)
        ident = keep.tile([P, P], F32)
        make_identity(nc, ident[:])

        w_raw = keep.tile([P, PACK, PROJ * EMBED], BF16)
        w_codes = keep.tile([P, PROJ * EMBED], U32, align_bytes=64)
        w_scales = keep.tile([P, PROJ * EMBED], U8, align_bytes=64)
        neg_codes = keep.tile([P, PROJ * NEG_COLS], U32, align_bytes=64)
        neg_scales = keep.tile([P, PROJ * NEG_COLS], U8, align_bytes=64)

        def load_weights(proj):
            cols = slice(proj * EMBED, (proj + 1) * EMBED)
            for u in range(2):
                nc.sync.dma_start(
                    out=w_raw[:, 2 * u : 2 * u + 2, cols],
                    in_=c_attn_w[u * 2 * P : (u + 1) * 2 * P, cols].rearrange("(q e) c -> q e c", e=2),
                )

        x_view = hidden_states.rearrange("b (i p r) k -> b i p r k", i=BANKS, r=PHASES)

        def load_quarter(b, i):
            x_raw = x_in.tile([P, PHASES, EMBED], BF16)
            nc.sync.dma_start(out=x_raw[:], in_=x_view[b, i])
            return x_raw

        def load_taps(proj, g, queue=nc.sync):
            taps = 2 * g + 1
            for head in range(HEADS_IN_GROUP):
                rows = slice(head * HEAD_DIM, (head + 1) * HEAD_DIM)
                queue.dma_start(out=tap_w_bf[rows, proj, g, 0:taps], in_=conv_w[proj][g - 1])
                queue.dma_start(
                    out=tap_b[rows, proj, g, 0:1], in_=conv_b[proj][g - 1].rearrange("(d o) -> d o", o=1)
                )

        def load_biases(proj, queue=nc.sync):
            with nc.allow_non_contiguous_dma(reason="one bias value per partition"):
                queue.dma_start(
                    out=bias_cols[:, proj, 0 : GROUPS - 1],
                    in_=c_attn_b[proj * EMBED + P : (proj + 1) * EMBED].rearrange("(g f) -> f g", f=P),
                )

        def load_bias_rows(proj):
            nc.sync.dma_start(
                out=bias_rows[:, proj, :],
                in_=c_attn_b[proj * EMBED : proj * EMBED + P].partition_broadcast(P),
            )

        load_biases(0, nc.scalar)
        load_taps(0, GROUP_ORDER[0][0], nc.scalar)
        batch_quarters = {0: [load_quarter(0, 0)]}
        load_weights(0)
        batch_quarters[0] += [load_quarter(0, i) for i in range(1, BANKS)]
        for g in GROUP_ORDER[0][1:]:
            load_taps(0, g)
        load_bias_rows(0)
        for proj in range(1, PROJ):
            load_weights(proj)
        for proj in range(1, PROJ):
            load_biases(proj)
            load_bias_rows(proj)
            for g in range(1, GROUPS):
                load_taps(proj, g)
        batch_quarters[1] = [load_quarter(1, i) for i in range(BANKS)]

        def make_constants(proj):
            gs = slice(1, GROUPS)
            nc.gpsimd.tensor_copy(out=tap_w[:, proj, gs, :], in_=tap_w_bf[:, proj, gs, :])
            nc.gpsimd.tensor_copy(out=bias_f[:, proj, gs], in_=bias_cols[:, proj, 0 : GROUPS - 1])
            for g in range(2, GROUPS):
                taps = 2 * g + 1
                nc.gpsimd.tensor_copy(out=tap_diff[:, proj, g, 0:1], in_=tap_w[:, proj, g, 0:1])
                nc.gpsimd.tensor_tensor(
                    out=tap_diff[:, proj, g, 1 : g + 1],
                    in0=tap_w[:, proj, g, 2:taps:2], in1=tap_w[:, proj, g, 1 : taps - 1 : 2], op=ALU.subtract,
                )
            width = GROUPS
            source = tap_w
            while width:
                nc.gpsimd.tensor_tensor(
                    out=base[:, proj, gs, 0:width], in0=source[:, proj, gs, 0:width],
                    in1=source[:, proj, gs, width : 2 * width], op=ALU.add,
                )
                source = base
                width //= 2
            nc.gpsimd.tensor_tensor(
                out=base[:, proj, gs, 0:1], in0=base[:, proj, gs, 0:1], in1=bias_f[:, proj, gs].unsqueeze(2), op=ALU.mult
            )
            nc.gpsimd.tensor_tensor(
                out=base[:, proj, gs, 0:1], in0=base[:, proj, gs, 0:1], in1=tap_b[:, proj, gs, 0:1], op=ALU.add
            )

        def make_corrections(proj):
            gs = slice(1, GROUPS)
            nc.gpsimd.tensor_copy(out=prefix[:, proj, gs, 0:1], in_=tap_w[:, proj, gs, 0:1])
            for n in range(1, 2 * GROUPS - 2):
                nc.gpsimd.tensor_tensor(
                    out=prefix[:, proj, gs, n : n + 1], in0=prefix[:, proj, gs, n - 1 : n],
                    in1=tap_w[:, proj, gs, n : n + 1], op=ALU.add,
                )
            for g in range(1, GROUPS):
                taps = 2 * g + 1
                for m in range(g):
                    n = taps - 2 - 2 * m
                    nc.gpsimd.tensor_scalar(
                        out=corr[:, proj, g, 0, m % 2, m // 2 : m // 2 + 1], in0=prefix[:, proj, g, n : n + 1],
                        scalar1=bias_f[:, proj, g : g + 1], scalar2=-1.0, op0=ALU.mult, op1=ALU.mult,
                    )
                    source, sign = (prefix[:, proj, g, 0:1], -1.0) if g == 1 else (tap_w[:, proj, g, n : n + 1], 1.0)
                    nc.gpsimd.tensor_scalar(
                        out=corr[:, proj, g, 1, m % 2, m // 2 : m // 2 + 1], in0=source,
                        scalar1=bias_f[:, proj, g : g + 1], scalar2=sign, op0=ALU.mult, op1=ALU.mult,
                    )

        make_constants(0)

        padded_tiles = [keep.tile([P, 2, PAD + PLACES], F32, name="padded_tile%d" % n) for n in range(PADDED_TILES)]
        for padded_tile in padded_tiles:
            nc.vector.memset(padded_tile[:, :, PAD - 1 : PAD], 0.0)

        w_stage = {}

        def group_weights(proj):
            cols = slice(proj * EMBED, (proj + 1) * EMBED)
            w_grouped = stage.tile([P, EMBED, PACK], BF16, align_bytes=64)
            nc.vector.tensor_copy(out=w_grouped[:], in_=w_raw[:, :, cols].rearrange("q j c -> q c j"))
            w_stage[proj] = w_grouped

        def group_some(proj, part):
            if part == 0:
                w_grouped = stage.tile([P, EMBED, PACK], BF16, align_bytes=64)
                w_stage[proj] = w_grouped
            first = part * P
            nc.scalar.copy(
                out=w_stage[proj][:, first : first + P, :],
                in_=w_raw[:, :, proj * EMBED + first : proj * EMBED + first + P].rearrange("q j c -> q c j"),
            )

        def negate_on_scalar(proj):
            negated = stage.tile([P, NEG_COLS, PACK], BF16, align_bytes=64)
            nc.scalar.activation(
                out=negated[:], in_=w_stage[proj][:, EMBED - NEG_COLS : EMBED, :], func=ACT.Copy, scale=-1.0
            )
            w_stage[proj, "neg"] = negated

        def negate_weights(proj):
            negated = stage.tile([P, NEG_COLS, PACK], BF16, align_bytes=64)
            nc.vector.tensor_scalar_mul(out=negated[:], in0=w_stage[proj][:, EMBED - NEG_COLS : EMBED, :], scalar1=-1.0)
            w_stage[proj, "neg"] = negated

        def quantise_weights(proj):
            cols = slice(proj * EMBED, (proj + 1) * EMBED)
            nc.vector.quantize_mx(
                out=w_codes[:, cols].bitcast(FP8X4), scales=w_scales[:, cols],
                in_=w_stage[proj][:].rearrange("q c j -> q (c j)"),
            )

        def quantise_negated(proj):
            cols = slice(proj * NEG_COLS, (proj + 1) * NEG_COLS)
            nc.vector.quantize_mx(
                out=neg_codes[:, cols].bitcast(FP8X4), scales=neg_scales[:, cols],
                in_=w_stage[proj, "neg"][:].rearrange("q c j -> q (c j)"),
            )

        x_codes = keep.tile([P, BATCH * SEQ], U32, align_bytes=64)
        x_scales = keep.tile([P, BATCH * SEQ], U8, align_bytes=64)
        x_stage = {}

        def turn_pair(b, n, copy):
            i, pair = n // 2, n % 2
            if n == 0:
                x_grouped = stage.tile([P, PHASES, PLACES, PACK], BF16, align_bytes=64, bufs=1)
                x_stage[b] = x_grouped
            words = x_stage[b][:].bitcast(F32)
            x_words = batch_quarters[b][i][:].bitcast(F32)
            turned = turn_psum.tile([P, 2, 2, P], F32, tag="turn")
            for j in range(2):
                for u in range(2):
                    nc.tensor.transpose(
                        turned[:, j, u, :], x_words[:, 2 * pair + j, u * P : (u + 1) * P], ident[:]
                    )
            first = i * P
            copy(
                out=words[:, 2 * pair : 2 * pair + 2, first : first + P, :],
                in_=turned[:].rearrange("q j u p -> q j p u"),
            )

        def quantise_tokens(b, r, half=None):
            if half is None:
                places = slice(0, PLACES)
            else:
                places = slice(half * 2 * P, (half + 1) * 2 * P)
            cols = slice(b * SEQ + r * PLACES + places.start, b * SEQ + r * PLACES + places.stop)
            nc.vector.quantize_mx(
                out=x_codes[:, cols].bitcast(FP8X4), scales=x_scales[:, cols],
                in_=x_stage[b][:, r, places, :].rearrange("q c j -> q (c j)"),
            )

        signals = []
        for b in range(BATCH):
            for proj in range(PROJ):
                plain = [(b, proj, 0, h) for h in range(2)]
                convs = []
                for g in GROUP_ORDER[b]:
                    convs += [(b, proj, g, name) for name in (["even", "odd"] if g == 1 else ["even", "odd", "diff"])]
                signals += plain + convs if b == 0 else convs + plain

        products = {}
        job_terms = {}
        padded_used = []

        def mx(out, lhs_codes, lhs_scales, lhs_cols, rhs_codes, rhs_scales, rhs_cols, start, stop):
            nc.tensor.matmul_mx(
                out=out,
                lhsT=lhs_codes[:, lhs_cols].bitcast(FP8X4), lhsT_scale=lhs_scales[:, lhs_cols],
                rhs=rhs_codes[:, rhs_cols].bitcast(FP8X4), rhs_scale=rhs_scales[:, rhs_cols],
                start=start, stop=stop,
            )

        def multiply(signal):
            b, proj, g, name = signal
            banks = []
            for h in range(2):
                bank = project_psum.tile([P, PLACES], F32, tag="project")
                if g == 0:
                    w_cols = slice(proj * EMBED, proj * EMBED + P)
                    for r in range(PHASES):
                        col = b * SEQ + r * PLACES + (2 * name + h) * P
                        mx(
                            bank[:, r * P : (r + 1) * P], x_codes, x_scales, slice(col, col + P),
                            w_codes, w_scales, w_cols, True, True,
                        )
                else:
                    first = proj * EMBED + g * P
                    w_cols = slice(first, first + P)
                    even_first = b * SEQ + 2 * h * PLACES
                    even = slice(even_first, even_first + PLACES)
                    odd = slice(even_first + PLACES, even_first + 2 * PLACES)
                    if name == "diff":
                        first = proj * NEG_COLS + (g - 2) * P
                        mx(bank[:], neg_codes, neg_scales, slice(first, first + P), x_codes, x_scales, even, True, False)
                        mx(bank[:], w_codes, w_scales, w_cols, x_codes, x_scales, odd, False, True)
                    else:
                        mx(bank[:], w_codes, w_scales, w_cols, x_codes, x_scales, even if name == "even" else odd, True, True)
                banks.append(bank)
            products[signal] = banks

        def weight(proj, g, back):
            n = 2 * g - back
            return tap_w[:, proj, g, n : n + 1]

        def diff_weight(proj, g, i):
            return tap_diff[:, proj, g, g - i : g - i + 1]

        def main_term(job, n):
            return job_terms[job][0][:, n]

        def padded_term(job, n):
            return job_terms[job][n][:, :, PAD:]

        def plan(signal):
            b, proj, g, name = signal
            job = signal[:3]
            bias = base[:, proj, g, 0:1]
            if g == 0:
                return [], []
            if g == 1:
                y0, y1 = main_term(job, 0), main_term(job, 1)
                if name == "even":
                    return (
                        [(y0, weight(proj, g, 0), bias), (y1, weight(proj, g, 1), bias)],
                        [(y0, 1, weight(proj, g, 2))],
                    )
                if LONE:
                    return (
                        [(job_terms[job][1][:], weight(proj, g, 0), None)],
                        [(y0, 1, weight(proj, g, 1)), (y1, 1, weight(proj, g, 2))],
                    )
                return [], [(y1, 0, weight(proj, g, 0)), (y0, 1, weight(proj, g, 1)), (y1, 1, weight(proj, g, 2))]
            if name == "even":
                term = main_term(job, 0)
                return [(term, weight(proj, g, 0), bias)], [(term, i, weight(proj, g, 2 * i)) for i in range(1, g + 1)]
            if name == "odd":
                term = padded_term(job, 1)
                return [(term, weight(proj, g, 1), None)], [(term, i, weight(proj, g, 2 * i + 1)) for i in range(1, g)]
            term = main_term(job, 1)
            if g not in SECOND_DIFF:
                return [(term, diff_weight(proj, g, 0), None)], [(term, i, diff_weight(proj, g, i)) for i in range(1, g + 1)]
            late = padded_term(job, 2)
            return (
                [(term, diff_weight(proj, g, 0), None), (late, diff_weight(proj, g, 1), None)],
                [(late if i % 2 else term, 2 * (i // 2), diff_weight(proj, g, i)) for i in range(2, g + 1)],
            )

        def open_job(signal):
            g, name = signal[2:]
            if g and name == "even":
                main = terms.tile([P, 2, 2, PLACES], F32, tag="main")
                mine = [main]
                if g == 1 and LONE:
                    lone = terms.tile([P, 2, PLACES], F32, tag="lone")
                    mine.append(lone)
                for n in range(g > 1 and 1 + (g in SECOND_DIFF)):
                    mine.append(padded_tiles[len(padded_used) % PADDED_TILES])
                    padded_used.append(signal)
                job_terms[signal[:3]] = mine

        def starts(signal):
            open_job(signal)

            def start(term, h, scale, bias):
                if bias is None:
                    nc.scalar.activation(out=term[:, h, :], in_=products[signal][h][:], func=ACT.Copy, scale=scale)
                else:
                    nc.scalar.activation(
                        out=term[:, h, :], in_=products[signal][h][:], func=ACT.Identity, scale=scale, bias=bias
                    )

            return [
                (lambda term=term, h=h, scale=scale, bias=bias: start(term, h, scale, bias))
                for h in range(2) for term, scale, bias in plan(signal)[0]
            ]

        def last_of_job(signal):
            return signal[3] == ("odd" if signal[2] == 1 else "diff")

        def add_taps(signal):
            b, proj, g, name = signal
            for h in range(2):
                taps = plan(signal)[1]
                for term, i, scalar in taps[::-1] if h else taps:
                    on, places = (h + i) % 2, (h + i) // 2
                    out = term[:, on, places:PLACES]
                    nc.vector.scalar_tensor_tensor(
                        out=out, in0=products[signal][h][:, 0 : PLACES - places], scalar=scalar, in1=out,
                        op0=ALU.mult, op1=ALU.add,
                    )

        def correct(job):
            early = job_terms[job][0][:, :, :, 0:2]
            nc.gpsimd.tensor_tensor(out=early, in0=early, in1=corr[:, job[1], job[2]], op=ALU.add)

        def store(b, proj, g, bank, result):
            heads = slice(g * HEADS_IN_GROUP, (g + 1) * HEADS_IN_GROUP)
            out_view = outs[proj][b, heads].rearrange("h (i p r) d -> i p h r d", i=BANKS, r=PHASES)
            nc.sync.dma_start(out=out_view[bank], in_=result[:])

        def add_plain(signal):
            b, proj, g, name = signal
            for h in range(2):
                result = results.tile([P, HEADS_IN_GROUP, PHASES, HEAD_DIM], F32, tag="result")
                nc.vector.tensor_tensor(
                    out=result[:],
                    in0=products[signal][h][:].rearrange("p (r h d) -> p h r d", r=PHASES, h=HEADS_IN_GROUP),
                    in1=bias_rows[:, proj, :].rearrange("p (h d) -> p h d", h=HEADS_IN_GROUP)
                    .unsqueeze(2).to_broadcast([P, HEADS_IN_GROUP, PHASES, HEAD_DIM]),
                    op=ALU.add,
                )
                store(b, proj, 0, 2 * name + h, result)

        def turn_terms(job, bank):
            g = job[2]
            by_token = turn_psum.tile([P, PHASES, P], F32, tag="turn")
            first = bank * P

            def here(term, h):
                return term[:, h, first : first + P]

            def one_back(tile, h):
                if h:
                    return tile[:, 0, PAD + first : PAD + first + P]
                return tile[:, 1, PAD - 1 + first : PAD - 1 + first + P]

            for r in range(PHASES):
                h, parity = divmod(r, 2)
                mine = job_terms[job]
                if g == 1:
                    parts = [here(main_term(job, parity), h)]
                    if parity and LONE:
                        parts.append(here(mine[1], h))
                elif parity == 0:
                    parts = [here(main_term(job, 0), h), one_back(mine[1], h)]
                else:
                    parts = [here(main_term(job, 0), h), here(padded_term(job, 1), h), here(main_term(job, 1), h)]
                    parts += [one_back(late, h) for late in mine[2:]]
                for n, part in enumerate(parts):
                    nc.tensor.matmul(
                        out=by_token[:, r, :], lhsT=part, rhs=ident[:], is_transpose=True,
                        start=(n == 0), stop=(n == len(parts) - 1),
                    )
            return by_token

        def copy_out(job, bank, by_token, copy=nc.scalar.copy):
            b, proj, g = job
            result = results.tile([P, HEADS_IN_GROUP, PHASES, HEAD_DIM], F32, tag="result")
            copy(out=result[:], in_=by_token[:].rearrange("p r (h d) -> p h r d", h=HEADS_IN_GROUP))
            store(b, proj, g, bank, result)

        group_weights(0)
        negate_weights(0)
        quantise_weights(0)
        quantise_negated(0)
        for n in range(2 * BANKS):
            turn_pair(0, n, nc.scalar.copy if n % 2 else nc.vector.tensor_copy)
            if n % 4 == 3:
                for r in range(PHASES):
                    quantise_tokens(0, r, n // 4)

        extras = [lambda: make_corrections(0)]
        for proj in range(1, PROJ):
            for parts in ((0,), (1,), (2, 3)):
                extras.append(lambda parts=parts, proj=proj: [group_some(proj, part) for part in parts])
            extras.append(lambda proj=proj: (negate_on_scalar(proj), quantise_weights(proj)))
            extras.append(lambda proj=proj: quantise_negated(proj))
            extras.append(lambda proj=proj: (make_constants(proj), make_corrections(proj)))
        for n in range(2 * BANKS):
            extras.append(lambda n=n: turn_pair(1, n, nc.scalar.copy))
        for r in range(PHASES):
            extras.append(lambda r=r: quantise_tokens(1, r))

        uncorrected = []
        turn_queue = []
        credit = 0
        for k in range(-2, len(signals)):
            begin = starts(signals[k + 1]) if 0 <= k + 1 < len(signals) else []
            ends = []
            if k >= 0:
                work = max(len(plan(signals[k])[1]), 1) * 2
                closing = k >= len(signals) - 2
                credit = CLOSING if closing else min(credit + work * CREDIT - len(begin), CAP)
                while turn_queue and turn_queue[0][0] < k - (1 if closing else LAG) and credit >= 1:
                    ends.append(turn_queue.pop(0)[1:])
                    credit -= 1
            turned = [turn_terms(*end) for end in ends[:2]]
            if k + 2 < len(signals):
                multiply(signals[k + 2])
            for n in range(max(len(begin), len(ends))):
                if n < len(begin):
                    begin[n]()
                if n < len(ends):
                    if n >= 2:
                        turned.append(turn_terms(*ends[n]))
                    copy_out(*ends[n], turned[n])
            if k >= 0:
                if signals[k][2] == 0:
                    add_plain(signals[k])
                else:
                    add_taps(signals[k])
                if uncorrected:
                    correct(uncorrected.pop(0))
                if last_of_job(signals[k]):
                    uncorrected.append(signals[k][:3])
                    turn_queue += [(k, signals[k][:3], bank) for bank in range(BANKS)]
                if extras and k >= 1:
                    extras.pop(0)()
        for job in uncorrected:
            correct(job)
        for k, job, bank in turn_queue:
            copy_out(job, bank, turn_terms(job, bank), nc.vector.tensor_copy if bank % 2 else nc.scalar.copy)
